import numpy as np
import ml_dtypes


def mxq(x, axis, fmt="e4m3"):
    dtype, down = {"e4m3": (ml_dtypes.float8_e4m3fn, 7), "e5m2": (ml_dtypes.float8_e5m2, 14)}[fmt]
    v = np.moveaxis(np.asarray(x, np.float32).astype(ml_dtypes.bfloat16).astype(np.float64), axis, -1)
    blocks = v.reshape(v.shape[:-1] + (-1, 32))
    amax = np.abs(blocks).max(-1, keepdims=True)
    byte = np.maximum(np.where(amax > 0, np.frexp(amax)[1] - 1 + 127, 0) - down, 1)
    scale = np.exp2(byte - 127.0)
    codes = (blocks / scale).astype(np.float32).astype(dtype).astype(np.float64)
    return np.moveaxis((codes * scale).reshape(v.shape), -1, axis)


WIDE = False


def mx_kscale(k):
    if not WIDE:
        return np.ones(k)
    levels = np.array([20, -20, 10, -10, 0])
    a = np.random.permutation(np.resize(levels, k // 512 * 4)).reshape(k // 512, 4)
    idx = np.arange(k)
    return np.exp2(a[idx // 512, idx % 128 // 32])


BF16 = ml_dtypes.bfloat16


def bf(x):
    return np.asarray(x, np.float32).astype(BF16)


def f64(x):
    return np.asarray(x).astype(np.float64)


B, S, IN, OUT, NBITS = 2, 1024, 1024, 512, 8
T = B * S
GSCALE = 64.0
EXPS = (2.0 ** np.arange(NBITS - 1, -1, -1)) / (2.0 ** NBITS - 1.0)


def _decode_bits(bits, sign_raw):
    return np.sum(bits * EXPS, axis=-1) * np.sign(sign_raw)


def setup_inputs():
    s = mx_kscale(T).reshape(B, S, 1)
    wint = np.random.randint(0, 2 ** NBITS, (OUT, IN))
    planes = (wint[:, :, None] >> np.arange(NBITS - 1, -1, -1)) & 1
    x = np.random.standard_normal((B, S, IN)) * s
    wsign = np.random.standard_normal((OUT, IN))
    scale = (1.7 / np.sqrt(IN)) * (1.0 + 0.1 * np.random.standard_normal(1))
    bbias = np.random.randint(0, 2, (OUT, NBITS))
    bsign = np.random.standard_normal(OUT)
    biasscale = 0.5 * (1.0 + 0.1 * np.random.standard_normal(1))
    g = np.random.standard_normal((B, S, OUT)) * np.exp2(np.random.randint(-12, 1, (B, S, 1))) * GSCALE / s
    return {"x": bf(x), "bweight": bf(planes), "wsign": bf(wsign), "scale": bf(scale),
            "bbias": bf(bbias), "bsign": bf(bsign), "biasscale": bf(biasscale),
            "grad_out": bf(g)}


def reference(x, bweight, wsign, scale, bbias, bsign, biasscale, grad_out):
    x2 = f64(x).reshape(T, IN)
    g2 = f64(grad_out).reshape(T, OUT)
    gw = mxq(g2, 0, "e5m2").T @ mxq(x2, 0, "e4m3")
    gd = gw * f64(scale)[0] * np.sign(f64(wsign))
    return gd[:, :, None] * EXPS

@@ -1,0 +1,195 @@
+from contextlib import ExitStack
+
+import concourse.mybir as mybir
+
+BF16 = mybir.dt.bfloat16
+F32 = mybir.dt.float32
+U32 = mybir.dt.uint32
+U8 = mybir.dt.uint8
+E4M3X4 = mybir.dt.float8_e4m3fn_x4
+E5M2X4 = mybir.dt.float8_e5m2_x4
+MULT = mybir.AluOpType.mult
+ACT = mybir.ActivationFunctionType
+
+P = 128
+PACK = 4
+K_PASS = P * PACK
+T = 2048
+IN = 1024
+OUT = 512
+NBITS = 8
+PASSES = T // K_PASS
+HALF = 512
+O_TILES = OUT // P
+SPLIT = 256
+PIECE = 256
+RUN = 4
+
+FLOPS = 2 * T * IN * OUT
+BYTES = 2 * (T * IN + T * OUT + OUT * IN + 1) + 4 * OUT * IN * NBITS
+
+
+def tile_bitlinear_kernel(
+    tc, x, bweight, wsign, scale, bbias, bsign, biasscale, grad_out, out
+):
+    nc = tc.nc
+    x2 = x.rearrange("b s i -> (b s) i")
+    g2 = grad_out.rearrange("b s o -> (b s) o")
+    ws_view = wsign.rearrange("(t p) i -> p t i", p=P)
+
+    with ExitStack() as ctx:
+        keep = ctx.enter_context(tc.tile_pool(name="keep", bufs=1))
+        rawp = ctx.enter_context(tc.tile_pool(name="rawp", bufs=1))
+        grpp = ctx.enter_context(tc.tile_pool(name="grpp", bufs=4))
+        gsp = ctx.enter_context(tc.tile_pool(name="gsp", bufs=3))
+        hp = ctx.enter_context(tc.tile_pool(name="hp", bufs=12))
+        psum = ctx.enter_context(tc.psum_pool(name="psum", bufs=1))
+        ctx.enter_context(tc.manual_schedule())
+
+        e4 = keep.tile([P, 4], F32, name="e4")
+        warm = keep.tile([P, 1], F32, name="warm")
+        sc_bf = keep.tile([P, 1], BF16, name="sc_bf")
+        sc = keep.tile([P, 1], F32, name="sc")
+        ws = keep.tile([P, O_TILES, IN], BF16, name="ws")
+        sgn = keep.tile([P, O_TILES, IN], BF16, name="sgn")
+        g_codes = keep.tile([P, PASSES, OUT], U32, name="g_codes", align_bytes=64)
+        g_scales = keep.tile([P, PASSES, OUT], U8, name="g_scales", align_bytes=64)
+        x_codes = keep.tile([P, PASSES, IN], U32, name="x_codes", align_bytes=64)
+        x_scales = keep.tile([P, PASSES, IN], U8, name="x_scales", align_bytes=64)
+        acc = [
+            [psum.tile([P, HALF], F32, name="acc%d%d" % (ot, h)) for h in range(2)]
+            for ot in range(O_TILES)
+        ]
+
+        nc.scalar.dma_start(out=sc_bf[:], in_=scale.partition_broadcast(P))
+        for j in range(4):
+            nc.vector.memset(e4[:, j : j + 1], 2.0 ** (NBITS - 1 - j))
+        nc.scalar.activation(out=warm[:], in_=e4[:, 0:1], func=ACT.Sign)
+
+        def load(name, rows):
+            raw = rawp.tile([P, PACK, HALF], BF16, name=name)
+            nc.sync.dma_start(out=raw[:], in_=rows.rearrange("(p j) w -> p j w", j=PACK))
+            return raw
+
+        def x_rows(c, h):
+            return x2[c * K_PASS : (c + 1) * K_PASS, h * HALF : (h + 1) * HALF]
+
+        raw_g = []
+        raw_x = [[], []]
+        for c in range(PASSES):
+            raw_g.append(load("raw_g%d" % c, g2[c * K_PASS : (c + 1) * K_PASS, :]))
+            raw_x[0].append(load("raw_xl%d" % c, x_rows(c, 0)))
+        nc.sync.dma_start(out=ws[:, :, 0:HALF], in_=ws_view[:, :, 0:HALF])
+        for c in range(PASSES):
+            raw_x[1].append(load("raw_xr%d" % c, x_rows(c, 1)))
+        nc.sync.dma_start(out=ws[:, :, HALF:IN], in_=ws_view[:, :, HALF:IN])
+
+        def regroup(raw):
+            grp = grpp.tile([P, HALF, PACK], BF16, name="grp", align_bytes=64)
+            for copy, lo, hi in (
+                (nc.vector.tensor_copy, 0, SPLIT),
+                (nc.scalar.copy, SPLIT, HALF),
+            ):
+                copy(
+                    out=grp[:, lo:hi, :].rearrange("p (c i) t -> p c t i", i=RUN),
+                    in_=raw[:, :, lo:hi].rearrange("p t (c i) -> p c t i", i=RUN),
+                )
+            return grp
+
+        def quantise_g(grp, c):
+            nc.vector.quantize_mx(
+                out=g_codes[:, c, :].bitcast(E5M2X4),
+                scales=g_scales[:, c, :],
+                in_=grp[:].rearrange("p w t -> p (w t)"),
+            )
+
+        def quantise_x(grp, c, h):
+            cols = slice(h * HALF, (h + 1) * HALF)
+            nc.vector.quantize_mx(
+                out=x_codes[:, c, cols].bitcast(E4M3X4),
+                scales=x_scales[:, c, cols],
+                in_=grp[:].rearrange("p w t -> p (w t)"),
+            )
+
+        def multiply(c, h):
+            cols = slice(h * HALF, (h + 1) * HALF)
+            for ot in range(O_TILES):
+                o_cols = slice(ot * P, (ot + 1) * P)
+                nc.tensor.matmul_mx(
+                    out=acc[ot][h][:],
+                    lhsT=g_codes[:, c, o_cols].bitcast(E5M2X4),
+                    lhsT_scale=g_scales[:, c, o_cols],
+                    rhs=x_codes[:, c, cols].bitcast(E4M3X4),
+                    rhs_scale=x_scales[:, c, cols],
+                    start=(c == 0),
+                    stop=(c == PASSES - 1),
+                )
+
+        def sign(ot, h):
+            cols = slice(h * HALF, (h + 1) * HALF)
+            nc.scalar.activation(out=sgn[:, ot, cols], in_=ws[:, ot, cols], func=ACT.Sign)
+
+        def unit(ot, h):
+            gs = gsp.tile([P, HALF], F32, name="gs")
+            nc.vector.scalar_tensor_tensor(
+                out=gs[:],
+                in0=acc[ot][h][:],
+                scalar=sc[:, 0:1],
+                in1=sgn[:, ot, h * HALF : (h + 1) * HALF],
+                op0=MULT,
+                op1=MULT,
+            )
+            for a in range(HALF // PIECE):
+                planes = hp.tile([P, PIECE, NBITS], F32, name="planes")
+                nc.vector.tensor_tensor(
+                    out=planes[:, :, 0:4],
+                    in0=gs[:, a * PIECE : (a + 1) * PIECE]
+                    .unsqueeze(2)
+                    .to_broadcast([P, PIECE, 4]),
+                    in1=e4[:].unsqueeze(1).to_broadcast([P, PIECE, 4]),
+                    op=MULT,
+                )
+                nc.scalar.activation(
+                    out=planes[:, :, 4:8], in_=planes[:, :, 0:4], func=ACT.Copy, scale=1.0 / 16.0
+                )
+                i0 = h * HALF + a * PIECE
+                nc.sync.dma_start(
+                    out=out[ot * P : (ot + 1) * P, i0 : i0 + PIECE, :], in_=planes[:]
+                )
+
+        grp_g = regroup(raw_g[0])
+        for c in range(PASSES):
+            grp_x = regroup(raw_x[0][c])
+            quantise_g(grp_g, c)
+            if c == 1:
+                nc.vector.tensor_scalar(
+                    out=sc[:], in0=sc_bf[:], scalar1=1.0 / 255.0, scalar2=None, op0=MULT
+                )
+            if c + 1 < PASSES:
+                grp_g = regroup(raw_g[c + 1])
+            quantise_x(grp_x, c, 0)
+            multiply(c, 0)
+        for ot in range(O_TILES):
+            sign(ot, 0)
+
+        unit(0, 0)
+        grp_r = [regroup(raw_x[1][0]), regroup(raw_x[1][1])]
+        unit(1, 0)
+        quantise_x(grp_r[0], 0, 1)
+        multiply(0, 1)
+        grp_r.append(regroup(raw_x[1][2]))
+        sign(0, 1)
+        sign(1, 1)
+        unit(2, 0)
+        quantise_x(grp_r[1], 1, 1)
+        multiply(1, 1)
+        grp_r.append(regroup(raw_x[1][3]))
+        sign(2, 1)
+        sign(3, 1)
+        quantise_x(grp_r[2], 2, 1)
+        multiply(2, 1)
+        unit(3, 0)
+        quantise_x(grp_r[3], 3, 1)
+        multiply(3, 1)
+        for ot in range(O_TILES):
+            unit(ot, 1)

@@ -24,6 +24,7 @@ O_TILES = OUT // P
 SPLIT = 256
 PIECE = 256
 RUN = 4
+WHOLE_PASSES = 2
 
 FLOPS = 2 * T * IN * OUT
 BYTES = 2 * (T * IN + T * OUT + OUT * IN + 1) + 4 * OUT * IN * NBITS
@@ -42,7 +43,7 @@ def tile_bitlinear_kernel(
         rawp = ctx.enter_context(tc.tile_pool(name="rawp", bufs=1))
         grpp = ctx.enter_context(tc.tile_pool(name="grpp", bufs=4))
         gsp = ctx.enter_context(tc.tile_pool(name="gsp", bufs=3))
-        hp = ctx.enter_context(tc.tile_pool(name="hp", bufs=12))
+        hp = ctx.enter_context(tc.tile_pool(name="hp", bufs=6))
         psum = ctx.enter_context(tc.psum_pool(name="psum", bufs=1))
         ctx.enter_context(tc.manual_schedule())
 
@@ -66,23 +67,27 @@ def tile_bitlinear_kernel(
             nc.vector.memset(e4[:, j : j + 1], 2.0 ** (NBITS - 1 - j))
         nc.scalar.activation(out=warm[:], in_=e4[:, 0:1], func=ACT.Sign)
 
-        def load(name, rows):
-            raw = rawp.tile([P, PACK, HALF], BF16, name=name)
+        def load(name, rows, width):
+            raw = rawp.tile([P, PACK, width], BF16, name=name)
             nc.sync.dma_start(out=raw[:], in_=rows.rearrange("(p j) w -> p j w", j=PACK))
             return raw
 
-        def x_rows(c, h):
-            return x2[c * K_PASS : (c + 1) * K_PASS, h * HALF : (h + 1) * HALF]
+        def rows_of(c):
+            return slice(c * K_PASS, (c + 1) * K_PASS)
 
         raw_g = []
-        raw_x = [[], []]
+        raw_x = []
         for c in range(PASSES):
-            raw_g.append(load("raw_g%d" % c, g2[c * K_PASS : (c + 1) * K_PASS, :]))
-            raw_x[0].append(load("raw_xl%d" % c, x_rows(c, 0)))
-        nc.sync.dma_start(out=ws[:, :, 0:HALF], in_=ws_view[:, :, 0:HALF])
-        for c in range(PASSES):
-            raw_x[1].append(load("raw_xr%d" % c, x_rows(c, 1)))
-        nc.sync.dma_start(out=ws[:, :, HALF:IN], in_=ws_view[:, :, HALF:IN])
+            raw_g.append(load("raw_g%d" % c, g2[rows_of(c), :], OUT))
+            if c < WHOLE_PASSES:
+                whole = load("raw_x%d" % c, x2[rows_of(c), :], IN)
+                raw_x.append([whole[:, :, 0:HALF], whole[:, :, HALF:IN]])
+            else:
+                raw_x.append([load("raw_xl%d" % c, x2[rows_of(c), 0:HALF], HALF)[:]])
+        nc.sync.dma_start(out=ws[:, 0:2, :], in_=ws_view[:, 0:2, :])
+        for c in range(WHOLE_PASSES, PASSES):
+            raw_x[c].append(load("raw_xr%d" % c, x2[rows_of(c), HALF:IN], HALF)[:])
+        nc.sync.dma_start(out=ws[:, 2:4, :], in_=ws_view[:, 2:4, :])
 
         def regroup(raw):
             grp = grpp.tile([P, HALF, PACK], BF16, name="grp", align_bytes=64)
@@ -110,9 +115,6 @@ def tile_bitlinear_kernel(
                 scales=x_scales[:, c, cols],
                 in_=grp[:].rearrange("p w t -> p (w t)"),
             )
-
-        def multiply(c, h):
-            cols = slice(h * HALF, (h + 1) * HALF)
             for ot in range(O_TILES):
                 o_cols = slice(ot * P, (ot + 1) * P)
                 nc.tensor.matmul_mx(
@@ -129,67 +131,76 @@ def tile_bitlinear_kernel(
             cols = slice(h * HALF, (h + 1) * HALF)
             nc.scalar.activation(out=sgn[:, ot, cols], in_=ws[:, ot, cols], func=ACT.Sign)
 
-        def unit(ot, h):
+        def unit(ot, h, gs_cuts, cuts, store_cuts):
             gs = gsp.tile([P, HALF], F32, name="gs")
-            nc.vector.scalar_tensor_tensor(
-                out=gs[:],
-                in0=acc[ot][h][:],
-                scalar=sc[:, 0:1],
-                in1=sgn[:, ot, h * HALF : (h + 1) * HALF],
-                op0=MULT,
-                op1=MULT,
-            )
-            for a in range(HALF // PIECE):
-                planes = hp.tile([P, PIECE, NBITS], F32, name="planes")
+            planes = hp.tile([P, HALF, NBITS], F32, name="planes")
+            scaled = 0
+            stored = 0
+            for lo, hi in zip(cuts[:-1], cuts[1:]):
+                while gs_cuts[scaled] < hi:
+                    a, b = gs_cuts[scaled], gs_cuts[scaled + 1]
+                    nc.vector.scalar_tensor_tensor(
+                        out=gs[:, a:b],
+                        in0=acc[ot][h][:, a:b],
+                        scalar=sc[:, 0:1],
+                        in1=sgn[:, ot, h * HALF + a : h * HALF + b],
+                        op0=MULT,
+                        op1=MULT,
+                    )
+                    scaled += 1
                 nc.vector.tensor_tensor(
-                    out=planes[:, :, 0:4],
-                    in0=gs[:, a * PIECE : (a + 1) * PIECE]
-                    .unsqueeze(2)
-                    .to_broadcast([P, PIECE, 4]),
-                    in1=e4[:].unsqueeze(1).to_broadcast([P, PIECE, 4]),
+                    out=planes[:, lo:hi, 0:4],
+                    in0=gs[:, lo:hi].unsqueeze(2).to_broadcast([P, hi - lo, 4]),
+                    in1=e4[:].unsqueeze(1).to_broadcast([P, hi - lo, 4]),
                     op=MULT,
                 )
                 nc.scalar.activation(
-                    out=planes[:, :, 4:8], in_=planes[:, :, 0:4], func=ACT.Copy, scale=1.0 / 16.0
+                    out=planes[:, lo:hi, 4:8],
+                    in_=planes[:, lo:hi, 0:4],
+                    func=ACT.Copy,
+                    scale=1.0 / 16.0,
                 )
-                i0 = h * HALF + a * PIECE
-                nc.sync.dma_start(
-                    out=out[ot * P : (ot + 1) * P, i0 : i0 + PIECE, :], in_=planes[:]
-                )
+                if hi in store_cuts:
+                    nc.sync.dma_start(
+                        out=out[ot * P : (ot + 1) * P, h * HALF + stored : h * HALF + hi, :],
+                        in_=planes[:, stored:hi, :],
+                    )
+                    stored = hi
 
         grp_g = regroup(raw_g[0])
-        for c in range(PASSES):
-            grp_x = regroup(raw_x[0][c])
+        grp_x = regroup(raw_x[0][0])
+        quantise_g(grp_g, 0)
+        grp_r = regroup(raw_x[0][1])
+        quantise_x(grp_x, 0, 0)
+        grp_g = regroup(raw_g[1])
+        quantise_x(grp_r, 0, 1)
+        nc.vector.tensor_scalar(
+            out=sc[:], in0=sc_bf[:], scalar1=1.0 / 255.0, scalar2=None, op0=MULT
+        )
+        for c in range(1, PASSES):
+            grp_x = regroup(raw_x[c][0])
             quantise_g(grp_g, c)
-            if c == 1:
-                nc.vector.tensor_scalar(
-                    out=sc[:], in0=sc_bf[:], scalar1=1.0 / 255.0, scalar2=None, op0=MULT
-                )
             if c + 1 < PASSES:
                 grp_g = regroup(raw_g[c + 1])
             quantise_x(grp_x, c, 0)
-            multiply(c, 0)
-        for ot in range(O_TILES):
-            sign(ot, 0)
 
-        unit(0, 0)
-        grp_r = [regroup(raw_x[1][0]), regroup(raw_x[1][1])]
-        unit(1, 0)
-        quantise_x(grp_r[0], 0, 1)
-        multiply(0, 1)
-        grp_r.append(regroup(raw_x[1][2]))
+        grp_r = regroup(raw_x[1][1])
+        sign(0, 0)
+        sign(1, 0)
+        unit(0, 0, (0, 128, 512), (0, 128, 256, 512), (128, 256, 512))
+        unit(1, 0, (0, 512), (0, 256, 512), (256, 512))
+        quantise_x(grp_r, 1, 1)
+        grp_r = regroup(raw_x[2][1])
+        sign(2, 0)
+        sign(3, 0)
+        unit(2, 0, (0, 512), (0, 256, 512), (256, 512))
+        quantise_x(grp_r, 2, 1)
+        grp_r = regroup(raw_x[3][1])
         sign(0, 1)
         sign(1, 1)
-        unit(2, 0)
-        quantise_x(grp_r[1], 1, 1)
-        multiply(1, 1)
-        grp_r.append(regroup(raw_x[1][3]))
+        unit(3, 0, (0, 512), (0, 256, 512), (256, 512))
+        quantise_x(grp_r, 3, 1)
         sign(2, 1)
         sign(3, 1)
-        quantise_x(grp_r[2], 2, 1)
-        multiply(2, 1)
-        unit(3, 0)
-        quantise_x(grp_r[3], 3, 1)
-        multiply(3, 1)
         for ot in range(O_TILES):
-            unit(ot, 1)
+            unit(ot, 1, (0, 512), (0, 256, 512), (512,))

@@ -43,7 +43,7 @@ def tile_bitlinear_kernel(
         rawp = ctx.enter_context(tc.tile_pool(name="rawp", bufs=1))
         grpp = ctx.enter_context(tc.tile_pool(name="grpp", bufs=4))
         gsp = ctx.enter_context(tc.tile_pool(name="gsp", bufs=3))
-        hp = ctx.enter_context(tc.tile_pool(name="hp", bufs=6))
+        hp = ctx.enter_context(tc.tile_pool(name="hp", bufs=12))
         psum = ctx.enter_context(tc.psum_pool(name="psum", bufs=1))
         ctx.enter_context(tc.manual_schedule())
 
@@ -84,10 +84,10 @@ def tile_bitlinear_kernel(
                 raw_x.append([whole[:, :, 0:HALF], whole[:, :, HALF:IN]])
             else:
                 raw_x.append([load("raw_xl%d" % c, x2[rows_of(c), 0:HALF], HALF)[:]])
-        nc.sync.dma_start(out=ws[:, 0:2, :], in_=ws_view[:, 0:2, :])
+        nc.sync.dma_start(out=ws[:, :, 0:HALF], in_=ws_view[:, :, 0:HALF])
         for c in range(WHOLE_PASSES, PASSES):
             raw_x[c].append(load("raw_xr%d" % c, x2[rows_of(c), HALF:IN], HALF)[:])
-        nc.sync.dma_start(out=ws[:, 2:4, :], in_=ws_view[:, 2:4, :])
+        nc.sync.dma_start(out=ws[:, :, HALF:IN], in_=ws_view[:, :, HALF:IN])
 
         def regroup(raw):
             grp = grpp.tile([P, HALF, PACK], BF16, name="grp", align_bytes=64)
@@ -131,11 +131,9 @@ def tile_bitlinear_kernel(
             cols = slice(h * HALF, (h + 1) * HALF)
             nc.scalar.activation(out=sgn[:, ot, cols], in_=ws[:, ot, cols], func=ACT.Sign)
 
-        def unit(ot, h, gs_cuts, cuts, store_cuts):
+        def unit(ot, h, gs_cuts, cuts):
             gs = gsp.tile([P, HALF], F32, name="gs")
-            planes = hp.tile([P, HALF, NBITS], F32, name="planes")
             scaled = 0
-            stored = 0
             for lo, hi in zip(cuts[:-1], cuts[1:]):
                 while gs_cuts[scaled] < hi:
                     a, b = gs_cuts[scaled], gs_cuts[scaled + 1]
@@ -148,24 +146,20 @@ def tile_bitlinear_kernel(
                         op1=MULT,
                     )
                     scaled += 1
+                planes = hp.tile([P, hi - lo, NBITS], F32, name="planes")
                 nc.vector.tensor_tensor(
-                    out=planes[:, lo:hi, 0:4],
+                    out=planes[:, :, 0:4],
                     in0=gs[:, lo:hi].unsqueeze(2).to_broadcast([P, hi - lo, 4]),
                     in1=e4[:].unsqueeze(1).to_broadcast([P, hi - lo, 4]),
                     op=MULT,
                 )
                 nc.scalar.activation(
-                    out=planes[:, lo:hi, 4:8],
-                    in_=planes[:, lo:hi, 0:4],
-                    func=ACT.Copy,
-                    scale=1.0 / 16.0,
+                    out=planes[:, :, 4:8], in_=planes[:, :, 0:4], func=ACT.Copy, scale=1.0 / 16.0
                 )
-                if hi in store_cuts:
-                    nc.sync.dma_start(
-                        out=out[ot * P : (ot + 1) * P, h * HALF + stored : h * HALF + hi, :],
-                        in_=planes[:, stored:hi, :],
-                    )
-                    stored = hi
+                nc.sync.dma_start(
+                    out=out[ot * P : (ot + 1) * P, h * HALF + lo : h * HALF + hi, :],
+                    in_=planes[:],
+                )
 
         grp_g = regroup(raw_g[0])
         grp_x = regroup(raw_x[0][0])
@@ -185,22 +179,20 @@ def tile_bitlinear_kernel(
             quantise_x(grp_x, c, 0)
 
         grp_r = regroup(raw_x[1][1])
-        sign(0, 0)
-        sign(1, 0)
-        unit(0, 0, (0, 128, 512), (0, 128, 256, 512), (128, 256, 512))
-        unit(1, 0, (0, 512), (0, 256, 512), (256, 512))
+        for ot in range(O_TILES):
+            sign(ot, 0)
+        unit(0, 0, (0, 128, 512), (0, 128, 256, 512))
+        unit(1, 0, (0, 512), (0, 256, 512))
         quantise_x(grp_r, 1, 1)
         grp_r = regroup(raw_x[2][1])
-        sign(2, 0)
-        sign(3, 0)
-        unit(2, 0, (0, 512), (0, 256, 512), (256, 512))
+        unit(2, 0, (0, 512), (0, 256, 512))
         quantise_x(grp_r, 2, 1)
         grp_r = regroup(raw_x[3][1])
         sign(0, 1)
         sign(1, 1)
-        unit(3, 0, (0, 512), (0, 256, 512), (256, 512))
+        unit(3, 0, (0, 512), (0, 256, 512))
         quantise_x(grp_r, 3, 1)
         sign(2, 1)
         sign(3, 1)
         for ot in range(O_TILES):
-            unit(ot, 1, (0, 512), (0, 256, 512), (512,))
+            unit(ot, 1, (0, 512), (0, 256, 512))

@@ -24,7 +24,7 @@ O_TILES = OUT // P
 SPLIT = 256
 PIECE = 256
 RUN = 4
-WHOLE_PASSES = 2
+WHOLE_PASSES = 0
 
 FLOPS = 2 * T * IN * OUT
 BYTES = 2 * (T * IN + T * OUT + OUT * IN + 1) + 4 * OUT * IN * NBITS
@@ -45,7 +45,6 @@ def tile_bitlinear_kernel(
         gsp = ctx.enter_context(tc.tile_pool(name="gsp", bufs=3))
         hp = ctx.enter_context(tc.tile_pool(name="hp", bufs=12))
         psum = ctx.enter_context(tc.psum_pool(name="psum", bufs=1))
-        ctx.enter_context(tc.manual_schedule())
 
         e4 = keep.tile([P, 4], F32, name="e4")
         warm = keep.tile([P, 1], F32, name="warm")
@@ -162,37 +161,33 @@ def tile_bitlinear_kernel(
                 )
 
         grp_g = regroup(raw_g[0])
-        grp_x = regroup(raw_x[0][0])
-        quantise_g(grp_g, 0)
-        grp_r = regroup(raw_x[0][1])
-        quantise_x(grp_x, 0, 0)
-        grp_g = regroup(raw_g[1])
-        quantise_x(grp_r, 0, 1)
-        nc.vector.tensor_scalar(
-            out=sc[:], in0=sc_bf[:], scalar1=1.0 / 255.0, scalar2=None, op0=MULT
-        )
-        for c in range(1, PASSES):
+        for c in range(PASSES):
             grp_x = regroup(raw_x[c][0])
             quantise_g(grp_g, c)
+            if c == 1:
+                nc.vector.tensor_scalar(
+                    out=sc[:], in0=sc_bf[:], scalar1=1.0 / 255.0, scalar2=None, op0=MULT
+                )
             if c + 1 < PASSES:
                 grp_g = regroup(raw_g[c + 1])
             quantise_x(grp_x, c, 0)
-
-        grp_r = regroup(raw_x[1][1])
         for ot in range(O_TILES):
             sign(ot, 0)
+
         unit(0, 0, (0, 128, 512), (0, 128, 256, 512))
+        grp_r = [regroup(raw_x[0][1]), regroup(raw_x[1][1])]
         unit(1, 0, (0, 512), (0, 256, 512))
-        quantise_x(grp_r, 1, 1)
-        grp_r = regroup(raw_x[2][1])
-        unit(2, 0, (0, 512), (0, 256, 512))
-        quantise_x(grp_r, 2, 1)
-        grp_r = regroup(raw_x[3][1])
+        quantise_x(grp_r[0], 0, 1)
+        grp_r.append(regroup(raw_x[2][1]))
         sign(0, 1)
         sign(1, 1)
-        unit(3, 0, (0, 512), (0, 256, 512))
-        quantise_x(grp_r, 3, 1)
+        unit(2, 0, (0, 512), (0, 256, 512))
+        quantise_x(grp_r[1], 1, 1)
+        grp_r.append(regroup(raw_x[3][1]))
         sign(2, 1)
         sign(3, 1)
+        quantise_x(grp_r[2], 2, 1)
+        unit(3, 0, (0, 512), (0, 256, 512))
+        quantise_x(grp_r[3], 3, 1)
         for ot in range(O_TILES):
             unit(ot, 1, (0, 512), (0, 256, 512))

@@ -43,10 +43,10 @@ def tile_bitlinear_kernel(
         rawp = ctx.enter_context(tc.tile_pool(name="rawp", bufs=1))
         grpp = ctx.enter_context(tc.tile_pool(name="grpp", bufs=4))
         gsp = ctx.enter_context(tc.tile_pool(name="gsp", bufs=3))
-        hp = ctx.enter_context(tc.tile_pool(name="hp", bufs=12))
+        hp = ctx.enter_context(tc.tile_pool(name="hp", bufs=6))
+        bigp = ctx.enter_context(tc.tile_pool(name="bigp", bufs=4))
         psum = ctx.enter_context(tc.psum_pool(name="psum", bufs=1))
 
-        e4 = keep.tile([P, 4], F32, name="e4")
         warm = keep.tile([P, 1], F32, name="warm")
         sc_bf = keep.tile([P, 1], BF16, name="sc_bf")
         sc = keep.tile([P, 1], F32, name="sc")
@@ -56,15 +56,20 @@ def tile_bitlinear_kernel(
         g_scales = keep.tile([P, PASSES, OUT], U8, name="g_scales", align_bytes=64)
         x_codes = keep.tile([P, PASSES, IN], U32, name="x_codes", align_bytes=64)
         x_scales = keep.tile([P, PASSES, IN], U8, name="x_scales", align_bytes=64)
-        acc = [
-            [psum.tile([P, HALF], F32, name="acc%d%d" % (ot, h)) for h in range(2)]
-            for ot in range(O_TILES)
-        ]
+        acc = [[psum.tile([P, HALF], F32, name="acc%d0" % ot)] for ot in range(O_TILES)]
+        for ot in range(O_TILES - 1):
+            acc[ot].append(psum.tile([P, HALF], F32, name="acc%d1" % ot))
+        e4 = psum.tile([P, HALF], F32, name="e4")
+        ones = keep.tile([P, P], BF16, name="ones")
+        table = keep.tile([P, 32], BF16, name="table")
 
         nc.scalar.dma_start(out=sc_bf[:], in_=scale.partition_broadcast(P))
+        nc.vector.memset(ones[:], 1.0)
+        nc.vector.memset(table[:], 0.0)
         for j in range(4):
-            nc.vector.memset(e4[:, j : j + 1], 2.0 ** (NBITS - 1 - j))
-        nc.scalar.activation(out=warm[:], in_=e4[:, 0:1], func=ACT.Sign)
+            nc.vector.memset(table[:, j : j + 1], 2.0 ** (-j))
+        nc.tensor.matmul(out=e4[:, 0:32], lhsT=ones[:], rhs=table[:], start=True, stop=True)
+        nc.scalar.activation(out=warm[:], in_=ones[:, 0:1], func=ACT.Sign)
 
         def load(name, rows, width):
             raw = rawp.tile([P, PACK, width], BF16, name=name)
@@ -83,17 +88,19 @@ def tile_bitlinear_kernel(
                 raw_x.append([whole[:, :, 0:HALF], whole[:, :, HALF:IN]])
             else:
                 raw_x.append([load("raw_xl%d" % c, x2[rows_of(c), 0:HALF], HALF)[:]])
-        nc.sync.dma_start(out=ws[:, :, 0:HALF], in_=ws_view[:, :, 0:HALF])
+        nc.sync.dma_start(out=ws[:, 0:2, :], in_=ws_view[:, 0:2, :])
         for c in range(WHOLE_PASSES, PASSES):
             raw_x[c].append(load("raw_xr%d" % c, x2[rows_of(c), HALF:IN], HALF)[:])
-        nc.sync.dma_start(out=ws[:, :, HALF:IN], in_=ws_view[:, :, HALF:IN])
+        nc.sync.dma_start(out=ws[:, 2:4, :], in_=ws_view[:, 2:4, :])
 
-        def regroup(raw):
+        def regroup(raw, split=SPLIT):
             grp = grpp.tile([P, HALF, PACK], BF16, name="grp", align_bytes=64)
             for copy, lo, hi in (
-                (nc.vector.tensor_copy, 0, SPLIT),
-                (nc.scalar.copy, SPLIT, HALF),
+                (nc.vector.tensor_copy, 0, split),
+                (nc.scalar.copy, split, HALF),
             ):
+                if lo == hi:
+                    continue
                 copy(
                     out=grp[:, lo:hi, :].rearrange("p (c i) t -> p c t i", i=RUN),
                     in_=raw[:, :, lo:hi].rearrange("p t (c i) -> p c t i", i=RUN),
@@ -130,8 +137,10 @@ def tile_bitlinear_kernel(
             cols = slice(h * HALF, (h + 1) * HALF)
             nc.scalar.activation(out=sgn[:, ot, cols], in_=ws[:, ot, cols], func=ACT.Sign)
 
-        def unit(ot, h, gs_cuts, cuts):
+        def unit(ot, h, gs_cuts, cuts, one_store):
             gs = gsp.tile([P, HALF], F32, name="gs")
+            if one_store:
+                whole = bigp.tile([P, HALF, NBITS], F32, name="whole")
             scaled = 0
             for lo, hi in zip(cuts[:-1], cuts[1:]):
                 while gs_cuts[scaled] < hi:
@@ -145,19 +154,41 @@ def tile_bitlinear_kernel(
                         op1=MULT,
                     )
                     scaled += 1
-                planes = hp.tile([P, hi - lo, NBITS], F32, name="planes")
+                if one_store:
+                    planes = whole[:, lo:hi, :]
+                else:
+                    piece = hp.tile([P, hi - lo, NBITS], F32, name="piece")
+                    planes = piece[:]
                 nc.vector.tensor_tensor(
                     out=planes[:, :, 0:4],
                     in0=gs[:, lo:hi].unsqueeze(2).to_broadcast([P, hi - lo, 4]),
-                    in1=e4[:].unsqueeze(1).to_broadcast([P, hi - lo, 4]),
+                    in1=e4[:, 0:4].unsqueeze(1).to_broadcast([P, hi - lo, 4]),
                     op=MULT,
                 )
-                nc.scalar.activation(
-                    out=planes[:, :, 4:8], in_=planes[:, :, 0:4], func=ACT.Copy, scale=1.0 / 16.0
-                )
+                if hi < HALF:
+                    nc.scalar.activation(
+                        out=planes[:, :, 4:8],
+                        in_=planes[:, :, 0:4],
+                        func=ACT.Copy,
+                        scale=1.0 / 16.0,
+                    )
+                else:
+                    nc.gpsimd.tensor_scalar(
+                        out=planes[:, :, 4:8],
+                        in0=planes[:, :, 0:4],
+                        scalar1=1.0 / 16.0,
+                        scalar2=1.0,
+                        op0=MULT,
+                        op1=MULT,
+                    )
+                if not one_store:
+                    nc.sync.dma_start(
+                        out=out[ot * P : (ot + 1) * P, h * HALF + lo : h * HALF + hi, :],
+                        in_=planes,
+                    )
+            if one_store:
                 nc.sync.dma_start(
-                    out=out[ot * P : (ot + 1) * P, h * HALF + lo : h * HALF + hi, :],
-                    in_=planes[:],
+                    out=out[ot * P : (ot + 1) * P, h * HALF : (h + 1) * HALF, :], in_=whole[:]
                 )
 
         grp_g = regroup(raw_g[0])
@@ -174,20 +205,21 @@ def tile_bitlinear_kernel(
         for ot in range(O_TILES):
             sign(ot, 0)
 
-        unit(0, 0, (0, 128, 512), (0, 128, 256, 512))
-        grp_r = [regroup(raw_x[0][1]), regroup(raw_x[1][1])]
-        unit(1, 0, (0, 512), (0, 256, 512))
+        unit(0, 0, (0, 128, 512), (0, 128, 256, 512), False)
+        acc[O_TILES - 1].append(psum.tile([P, HALF], F32, name="acc31", tag="acc00"))
+        grp_r = [regroup(raw_x[0][1], 0), regroup(raw_x[1][1], 0)]
+        unit(1, 0, (0, 512), (0, 256, 512), False)
         quantise_x(grp_r[0], 0, 1)
-        grp_r.append(regroup(raw_x[2][1]))
+        grp_r.append(regroup(raw_x[2][1], 0))
         sign(0, 1)
         sign(1, 1)
-        unit(2, 0, (0, 512), (0, 256, 512))
+        unit(2, 0, (0, 512), (0, 256, 512), False)
         quantise_x(grp_r[1], 1, 1)
-        grp_r.append(regroup(raw_x[3][1]))
+        grp_r.append(regroup(raw_x[3][1], 0))
         sign(2, 1)
         sign(3, 1)
         quantise_x(grp_r[2], 2, 1)
-        unit(3, 0, (0, 512), (0, 256, 512))
+        unit(3, 0, (0, 512), (0, 256, 512), True)
         quantise_x(grp_r[3], 3, 1)
         for ot in range(O_TILES):
-            unit(ot, 1, (0, 512), (0, 256, 512))
+            unit(ot, 1, (0, 512), (0, 256, 512), True)

@@ -49,7 +49,7 @@ def tile_bitlinear_kernel(
 
         warm = keep.tile([P, 1], F32, name="warm")
         sc_bf = keep.tile([P, 1], BF16, name="sc_bf")
-        sc = keep.tile([P, 1], F32, name="sc")
+        pw = keep.tile([P, 4], BF16, name="pw")
         ws = keep.tile([P, O_TILES, IN], BF16, name="ws")
         sgn = keep.tile([P, O_TILES, IN], BF16, name="sgn")
         g_codes = keep.tile([P, PASSES, OUT], U32, name="g_codes", align_bytes=64)
@@ -63,11 +63,14 @@ def tile_bitlinear_kernel(
         ones = keep.tile([P, P], BF16, name="ones")
         table = keep.tile([P, 32], BF16, name="table")
 
-        nc.scalar.dma_start(out=sc_bf[:], in_=scale.partition_broadcast(P))
+        nc.scalar.dma_start(out=sc_bf[0:1, 0:1], in_=scale.unsqueeze(0))
         nc.vector.memset(ones[:], 1.0)
         nc.vector.memset(table[:], 0.0)
         for j in range(4):
-            nc.vector.memset(table[:, j : j + 1], 2.0 ** (-j))
+            nc.vector.memset(pw[:, j : j + 1], 2.0 ** (7 - j))
+        nc.vector.tensor_scalar(
+            out=table[0:1, 0:4], in0=pw[0:1, 0:4], scalar1=sc_bf[0:1, 0:1], scalar2=None, op0=MULT
+        )
         nc.tensor.matmul(out=e4[:, 0:32], lhsT=ones[:], rhs=table[:], start=True, stop=True)
         nc.scalar.activation(out=warm[:], in_=ones[:, 0:1], func=ACT.Sign)
 
@@ -148,7 +151,7 @@ def tile_bitlinear_kernel(
                     nc.vector.scalar_tensor_tensor(
                         out=gs[:, a:b],
                         in0=acc[ot][h][:, a:b],
-                        scalar=sc[:, 0:1],
+                        scalar=1.0 / 255.0,
                         in1=sgn[:, ot, h * HALF + a : h * HALF + b],
                         op0=MULT,
                         op1=MULT,
@@ -195,10 +198,6 @@ def tile_bitlinear_kernel(
         for c in range(PASSES):
             grp_x = regroup(raw_x[c][0])
             quantise_g(grp_g, c)
-            if c == 1:
-                nc.vector.tensor_scalar(
-                    out=sc[:], in0=sc_bf[:], scalar1=1.0 / 255.0, scalar2=None, op0=MULT
-                )
             if c + 1 < PASSES:
                 grp_g = regroup(raw_g[c + 1])
             quantise_x(grp_x, c, 0)

@@ -1,6 +1,7 @@
 from contextlib import ExitStack
 
 import concourse.mybir as mybir
+from concourse.masks import make_identity
 
 BF16 = mybir.dt.bfloat16
 F32 = mybir.dt.float32
@@ -57,11 +58,11 @@ def tile_bitlinear_kernel(
         x_codes = keep.tile([P, PASSES, IN], U32, name="x_codes", align_bytes=64)
         x_scales = keep.tile([P, PASSES, IN], U8, name="x_scales", align_bytes=64)
         acc = [[psum.tile([P, HALF], F32, name="acc%d0" % ot)] for ot in range(O_TILES)]
-        for ot in range(O_TILES - 1):
-            acc[ot].append(psum.tile([P, HALF], F32, name="acc%d1" % ot))
         e4 = psum.tile([P, HALF], F32, name="e4")
         ones = keep.tile([P, P], BF16, name="ones")
         table = keep.tile([P, 32], BF16, name="table")
+        ident = keep.tile([P, P], BF16, name="ident")
+        make_identity(nc, ident[:])
 
         nc.scalar.dma_start(out=sc_bf[0:1, 0:1], in_=scale.unsqueeze(0))
         nc.vector.memset(ones[:], 1.0)
@@ -107,6 +108,25 @@ def tile_bitlinear_kernel(
                 copy(
                     out=grp[:, lo:hi, :].rearrange("p (c i) t -> p c t i", i=RUN),
                     in_=raw[:, :, lo:hi].rearrange("p t (c i) -> p c t i", i=RUN),
+                )
+            return grp
+
+        def regroup_on_tensor(raw, banks):
+            grp = grpp.tile([P, HALF, PACK], BF16, name="grp", align_bytes=64)
+            for part, bank in enumerate(banks):
+                turned = psum.tile([P, 2 * HALF], BF16, name="turned", tag=bank)
+                for q in range(2):
+                    lo = part * 256 + q * P
+                    nc.tensor.matmul(
+                        out=turned[:, q * HALF : (q + 1) * HALF],
+                        lhsT=ident[:],
+                        rhs=raw[:, :, lo : lo + P].rearrange("p t c -> p c t"),
+                        start=True,
+                        stop=True,
+                    )
+                nc.scalar.copy(
+                    out=grp[:, part * 256 : (part + 1) * 256, :].rearrange("p w t -> p (w t)"),
+                    in_=turned[:],
                 )
             return grp
 
@@ -204,12 +224,18 @@ def tile_bitlinear_kernel(
         for ot in range(O_TILES):
             sign(ot, 0)
 
-        unit(0, 0, (0, 128, 512), (0, 128, 256, 512), False)
-        acc[O_TILES - 1].append(psum.tile([P, HALF], F32, name="acc31", tag="acc00"))
-        grp_r = [regroup(raw_x[0][1], 0), regroup(raw_x[1][1], 0)]
+        unit(0, 0, (0, 64, 512), (0, 64, 128, 256, 512), False)
+        acc31 = psum.tile([P, HALF], F32, name="acc31", tag="acc00")
+        grp_r = [
+            regroup_on_tensor(raw_x[0][1], ("acc01", "acc11")),
+            regroup_on_tensor(raw_x[1][1], ("acc21", "acc01")),
+        ]
         unit(1, 0, (0, 512), (0, 256, 512), False)
+        grp_r.append(regroup_on_tensor(raw_x[2][1], ("acc11", "acc21")))
+        for ot in range(O_TILES - 1):
+            acc[ot].append(psum.tile([P, HALF], F32, name="acc%d1" % ot))
+        acc[O_TILES - 1].append(acc31)
         quantise_x(grp_r[0], 0, 1)
-        grp_r.append(regroup(raw_x[2][1], 0))
         sign(0, 1)
         sign(1, 1)
         unit(2, 0, (0, 512), (0, 256, 512), False)

@@ -22,10 +22,10 @@ NBITS = 8
 PASSES = T // K_PASS
 HALF = 512
 O_TILES = OUT // P
-SPLIT = 256
-PIECE = 256
 RUN = 4
-WHOLE_PASSES = 0
+HEAD = (("g", 0), ("x", 0), ("g", 1), ("x", 1), ("x", 2), ("x", 3))
+RIGHT_BANKS = (5, 6, 7, 0)
+WHOLE = 3
 
 FLOPS = 2 * T * IN * OUT
 BYTES = 2 * (T * IN + T * OUT + OUT * IN + 1) + 4 * OUT * IN * NBITS
@@ -50,15 +50,18 @@ def tile_bitlinear_kernel(
 
         warm = keep.tile([P, 1], F32, name="warm")
         sc_bf = keep.tile([P, 1], BF16, name="sc_bf")
-        pw = keep.tile([P, 4], BF16, name="pw")
+        pw = keep.tile([P, NBITS], BF16, name="pw")
         ws = keep.tile([P, O_TILES, IN], BF16, name="ws")
         sgn = keep.tile([P, O_TILES, IN], BF16, name="sgn")
         g_codes = keep.tile([P, PASSES, OUT], U32, name="g_codes", align_bytes=64)
         g_scales = keep.tile([P, PASSES, OUT], U8, name="g_scales", align_bytes=64)
         x_codes = keep.tile([P, PASSES, IN], U32, name="x_codes", align_bytes=64)
         x_scales = keep.tile([P, PASSES, IN], U8, name="x_scales", align_bytes=64)
-        acc = [[psum.tile([P, HALF], F32, name="acc%d0" % ot)] for ot in range(O_TILES)]
-        e4 = psum.tile([P, HALF], F32, name="e4")
+        acc = [
+            [psum.tile([P, HALF], F32, name="acc%d0" % ot, tag="bank%d" % ot), None]
+            for ot in range(O_TILES)
+        ]
+        e8 = psum.tile([P, HALF], F32, name="e8", tag="bank4")
         ones = keep.tile([P, P], BF16, name="ones")
         table = keep.tile([P, 32], BF16, name="table")
         ident = keep.tile([P, P], BF16, name="ident")
@@ -67,12 +70,12 @@ def tile_bitlinear_kernel(
         nc.scalar.dma_start(out=sc_bf[0:1, 0:1], in_=scale.unsqueeze(0))
         nc.vector.memset(ones[:], 1.0)
         nc.vector.memset(table[:], 0.0)
-        for j in range(4):
+        for j in range(NBITS):
             nc.vector.memset(pw[:, j : j + 1], 2.0 ** (7 - j))
         nc.vector.tensor_scalar(
-            out=table[0:1, 0:4], in0=pw[0:1, 0:4], scalar1=sc_bf[0:1, 0:1], scalar2=None, op0=MULT
+            out=table[0:1, 0:NBITS], in0=pw[0:1, 0:NBITS], scalar1=sc_bf[0:1, 0:1], scalar2=None, op0=MULT
         )
-        nc.tensor.matmul(out=e4[:, 0:32], lhsT=ones[:], rhs=table[:], start=True, stop=True)
+        nc.tensor.matmul(out=e8[:, 0:32], lhsT=ones[:], rhs=table[:], start=True, stop=True)
         nc.scalar.activation(out=warm[:], in_=ones[:, 0:1], func=ACT.Sign)
 
         def load(name, rows, width):
@@ -83,32 +86,38 @@ def tile_bitlinear_kernel(
         def rows_of(c):
             return slice(c * K_PASS, (c + 1) * K_PASS)
 
-        raw_g = []
-        raw_x = []
-        for c in range(PASSES):
-            raw_g.append(load("raw_g%d" % c, g2[rows_of(c), :], OUT))
-            if c < WHOLE_PASSES:
-                whole = load("raw_x%d" % c, x2[rows_of(c), :], IN)
-                raw_x.append([whole[:, :, 0:HALF], whole[:, :, HALF:IN]])
-            else:
-                raw_x.append([load("raw_xl%d" % c, x2[rows_of(c), 0:HALF], HALF)[:]])
-        nc.sync.dma_start(out=ws[:, 0:2, :], in_=ws_view[:, 0:2, :])
-        for c in range(WHOLE_PASSES, PASSES):
-            raw_x[c].append(load("raw_xr%d" % c, x2[rows_of(c), HALF:IN], HALF)[:])
-        nc.sync.dma_start(out=ws[:, 2:4, :], in_=ws_view[:, 2:4, :])
+        raw_g = [None] * PASSES
+        raw_x = [[None, None] for c in range(PASSES)]
 
-        def regroup(raw, split=SPLIT):
+        def load_g(c):
+            raw_g[c] = load("raw_g%d" % c, g2[rows_of(c), :], OUT)[:]
+
+        def load_x(c):
+            if c >= WHOLE:
+                whole = load("raw_x%d" % c, x2[rows_of(c), :], IN)
+                raw_x[c] = [whole[:, :, 0:HALF], whole[:, :, HALF:IN]]
+            else:
+                raw_x[c][0] = load("raw_xl%d" % c, x2[rows_of(c), 0:HALF], HALF)[:]
+
+        for kind, c in HEAD:
+            (load_g if kind == "g" else load_x)(c)
+        load_g(2)
+        load_g(3)
+        nc.sync.dma_start(out=ws[:, 0:1, :], in_=ws_view[:, 0:1, :])
+        nc.sync.dma_start(out=ws[:, 1:4, :], in_=ws_view[:, 1:4, :])
+        for c in range(WHOLE):
+            raw_x[c][1] = load("raw_xr%d" % c, x2[rows_of(c), HALF:IN], HALF)[:]
+
+        def interleave(copy, grp, raw, lo, hi):
+            copy(
+                out=grp[:, lo:hi, :].rearrange("p (c i) t -> p c t i", i=RUN),
+                in_=raw[:, :, lo:hi].rearrange("p t (c i) -> p c t i", i=RUN),
+            )
+
+        def regroup(raw, shares):
             grp = grpp.tile([P, HALF, PACK], BF16, name="grp", align_bytes=64)
-            for copy, lo, hi in (
-                (nc.vector.tensor_copy, 0, split),
-                (nc.scalar.copy, split, HALF),
-            ):
-                if lo == hi:
-                    continue
-                copy(
-                    out=grp[:, lo:hi, :].rearrange("p (c i) t -> p c t i", i=RUN),
-                    in_=raw[:, :, lo:hi].rearrange("p t (c i) -> p c t i", i=RUN),
-                )
+            for copy, lo, hi in shares:
+                interleave(copy, grp, raw, lo, hi)
             return grp
 
         def regroup_on_tensor(raw, banks):
@@ -130,11 +139,11 @@ def tile_bitlinear_kernel(
                 )
             return grp
 
-        def quantise_g(grp, c):
+        def quantise_g(grp, c, lo, hi):
             nc.vector.quantize_mx(
-                out=g_codes[:, c, :].bitcast(E5M2X4),
-                scales=g_scales[:, c, :],
-                in_=grp[:].rearrange("p w t -> p (w t)"),
+                out=g_codes[:, c, lo:hi].bitcast(E5M2X4),
+                scales=g_scales[:, c, lo:hi],
+                in_=grp[:, lo:hi, :].rearrange("p w t -> p (w t)"),
             )
 
         def quantise_x(grp, c, h):
@@ -144,7 +153,10 @@ def tile_bitlinear_kernel(
                 scales=x_scales[:, c, cols],
                 in_=grp[:].rearrange("p w t -> p (w t)"),
             )
-            for ot in range(O_TILES):
+
+        def multiply(c, h, o_tiles, first, last):
+            cols = slice(h * HALF, (h + 1) * HALF)
+            for ot in o_tiles:
                 o_cols = slice(ot * P, (ot + 1) * P)
                 nc.tensor.matmul_mx(
                     out=acc[ot][h][:],
@@ -152,99 +164,163 @@ def tile_bitlinear_kernel(
                     lhsT_scale=g_scales[:, c, o_cols],
                     rhs=x_codes[:, c, cols].bitcast(E4M3X4),
                     rhs_scale=x_scales[:, c, cols],
-                    start=(c == 0),
-                    stop=(c == PASSES - 1),
+                    start=(c == first),
+                    stop=(c == last),
                 )
 
-        def sign(ot, h):
-            cols = slice(h * HALF, (h + 1) * HALF)
+        def sign(ot, h, lo=0, hi=HALF):
+            cols = slice(h * HALF + lo, h * HALF + hi)
             nc.scalar.activation(out=sgn[:, ot, cols], in_=ws[:, ot, cols], func=ACT.Sign)
 
-        def unit(ot, h, gs_cuts, cuts, one_store):
+        def scaled(gs, ot, h, lo, hi):
+            nc.vector.scalar_tensor_tensor(
+                out=gs[:, lo:hi],
+                in0=acc[ot][h][:, lo:hi],
+                scalar=1.0 / 255.0,
+                in1=sgn[:, ot, h * HALF + lo : h * HALF + hi],
+                op0=MULT,
+                op1=MULT,
+            )
+
+        def expand(planes, gs, lo, hi, count):
+            nc.vector.tensor_tensor(
+                out=planes[:, :, 0:count],
+                in0=gs[:, lo:hi].unsqueeze(2).to_broadcast([P, hi - lo, count]),
+                in1=e8[:, 0:count].unsqueeze(1).to_broadcast([P, hi - lo, count]),
+                op=MULT,
+            )
+
+        def low_planes(planes, on_gpsimd):
+            if on_gpsimd:
+                nc.gpsimd.tensor_scalar(
+                    out=planes[:, :, 4:8],
+                    in0=planes[:, :, 0:4],
+                    scalar1=1.0 / 16.0,
+                    scalar2=1.0,
+                    op0=MULT,
+                    op1=MULT,
+                )
+            else:
+                nc.scalar.activation(
+                    out=planes[:, :, 4:8], in_=planes[:, :, 0:4], func=ACT.Copy, scale=1.0 / 16.0
+                )
+
+        def store(planes, ot, h, lo, hi):
+            nc.sync.dma_start(
+                out=out[ot * P : (ot + 1) * P, h * HALF + lo : h * HALF + hi, :], in_=planes
+            )
+
+        def piece_of(gs, ot, h, lo, hi, where):
+            piece = hp.tile([P, hi - lo, NBITS], F32, name="piece")
+            expand(piece[:], gs, lo, hi, 4)
+            low_planes(piece[:], where == "gpsimd")
+            store(piece[:], ot, h, lo, hi)
+
+        def unit(ot, h, pieces, one_store, gs_cuts=(0, HALF)):
             gs = gsp.tile([P, HALF], F32, name="gs")
             if one_store:
                 whole = bigp.tile([P, HALF, NBITS], F32, name="whole")
-            scaled = 0
-            for lo, hi in zip(cuts[:-1], cuts[1:]):
-                while gs_cuts[scaled] < hi:
-                    a, b = gs_cuts[scaled], gs_cuts[scaled + 1]
-                    nc.vector.scalar_tensor_tensor(
-                        out=gs[:, a:b],
-                        in0=acc[ot][h][:, a:b],
-                        scalar=1.0 / 255.0,
-                        in1=sgn[:, ot, h * HALF + a : h * HALF + b],
-                        op0=MULT,
-                        op1=MULT,
-                    )
-                    scaled += 1
+            n = 0
+            for lo, hi, where in pieces:
+                while gs_cuts[n] < hi:
+                    scaled(gs, ot, h, gs_cuts[n], gs_cuts[n + 1])
+                    n += 1
                 if one_store:
                     planes = whole[:, lo:hi, :]
                 else:
                     piece = hp.tile([P, hi - lo, NBITS], F32, name="piece")
                     planes = piece[:]
-                nc.vector.tensor_tensor(
-                    out=planes[:, :, 0:4],
-                    in0=gs[:, lo:hi].unsqueeze(2).to_broadcast([P, hi - lo, 4]),
-                    in1=e4[:, 0:4].unsqueeze(1).to_broadcast([P, hi - lo, 4]),
-                    op=MULT,
-                )
-                if hi < HALF:
-                    nc.scalar.activation(
-                        out=planes[:, :, 4:8],
-                        in_=planes[:, :, 0:4],
-                        func=ACT.Copy,
-                        scale=1.0 / 16.0,
-                    )
+                if where == "vector":
+                    expand(planes, gs, lo, hi, NBITS)
                 else:
-                    nc.gpsimd.tensor_scalar(
-                        out=planes[:, :, 4:8],
-                        in0=planes[:, :, 0:4],
-                        scalar1=1.0 / 16.0,
-                        scalar2=1.0,
-                        op0=MULT,
-                        op1=MULT,
-                    )
+                    expand(planes, gs, lo, hi, 4)
+                    low_planes(planes, where == "gpsimd")
                 if not one_store:
-                    nc.sync.dma_start(
-                        out=out[ot * P : (ot + 1) * P, h * HALF + lo : h * HALF + hi, :],
-                        in_=planes,
-                    )
+                    store(planes, ot, h, lo, hi)
             if one_store:
-                nc.sync.dma_start(
-                    out=out[ot * P : (ot + 1) * P, h * HALF : (h + 1) * HALF, :], in_=whole[:]
-                )
+                store(whole[:], ot, h, 0, HALF)
 
-        grp_g = regroup(raw_g[0])
-        for c in range(PASSES):
-            grp_x = regroup(raw_x[c][0])
-            quantise_g(grp_g, c)
-            if c + 1 < PASSES:
-                grp_g = regroup(raw_g[c + 1])
-            quantise_x(grp_x, c, 0)
-        for ot in range(O_TILES):
-            sign(ot, 0)
+        vector_copy = nc.vector.tensor_copy
+        scalar_copy = nc.scalar.copy
+        both = ((vector_copy, 0, 256), (scalar_copy, 256, HALF))
 
-        unit(0, 0, (0, 64, 512), (0, 64, 128, 256, 512), False)
-        acc31 = psum.tile([P, HALF], F32, name="acc31", tag="acc00")
-        grp_r = [
-            regroup_on_tensor(raw_x[0][1], ("acc01", "acc11")),
-            regroup_on_tensor(raw_x[1][1], ("acc21", "acc01")),
-        ]
-        unit(1, 0, (0, 512), (0, 256, 512), False)
-        grp_r.append(regroup_on_tensor(raw_x[2][1], ("acc11", "acc21")))
+        pending = []
+
+        def prepare(kind, c):
+            raw = raw_g[c] if kind == "g" else raw_x[c][0]
+            pending.append((kind, c, regroup(raw, both)))
+
+        def finish():
+            kind, c, grp = pending.pop(0)
+            if kind == "g":
+                quantise_g(grp, c, 0, OUT)
+            else:
+                quantise_x(grp, c, 0)
+            if kind == "x" and c < 2:
+                multiply(c, 0, range(O_TILES), 0, PASSES - 1)
+
+        for i, (kind, c) in enumerate(HEAD):
+            prepare(kind, c)
+            if i > 0:
+                finish()
+        last = PASSES - 1
+        grp_g = [None, None]
+        grp_g[0] = regroup(raw_g[2], ((vector_copy, 0, 128), (scalar_copy, 128, HALF)))
+        finish()
+        quantise_g(grp_g[0], 2, 0, 128)
+        multiply(2, 0, (0,), 0, last)
+        sign(0, 0)
+        grp_g[1] = regroup(raw_g[3], ((vector_copy, 0, 128), (scalar_copy, 256, 384)))
+        quantise_g(grp_g[1], 3, 0, 128)
+        multiply(3, 0, (0,), 0, last)
+        interleave(vector_copy, grp_g[1], raw_g[3], 128, 256)
+        quantise_g(grp_g[0], 2, 128, 256)
+        gs = gsp.tile([P, HALF], F32, name="gs")
+        scaled(gs, 0, 0, 0, 64)
+        quantise_g(grp_g[1], 3, 128, 256)
+        multiply(2, 0, (1,), 0, last)
+        multiply(3, 0, (1,), 0, last)
+        piece_of(gs, 0, 0, 0, 64, "scalar")
+        scaled(gs, 0, 0, 64, 256)
+        piece_of(gs, 0, 0, 64, 128, "scalar")
+        piece_of(gs, 0, 0, 128, 256, "scalar")
+        sign(1, 0)
+        scaled(gs, 0, 0, 256, 512)
+        piece_of(gs, 0, 0, 256, 512, "scalar")
+        unit(1, 0, ((0, 256, "scalar"), (256, 512, "gpsimd")), False)
+        interleave(scalar_copy, grp_g[1], raw_g[3], 384, HALF)
+        grp_r = [None] * PASSES
+        grp_r[2] = regroup_on_tensor(raw_x[2][1], ("bank7", "bank0"))
+        sign(2, 0)
+        for c in (2, 3):
+            quantise_g(grp_g[c - 2], c, 256, 512)
+        for ot in (2, 3):
+            for c in (2, 3):
+                multiply(c, 0, (ot,), 0, last)
         for ot in range(O_TILES - 1):
-            acc[ot].append(psum.tile([P, HALF], F32, name="acc%d1" % ot))
-        acc[O_TILES - 1].append(acc31)
-        quantise_x(grp_r[0], 0, 1)
+            acc[ot][1] = psum.tile([P, HALF], F32, name="acc%d1" % ot, tag="bank%d" % RIGHT_BANKS[ot])
+        quantise_x(grp_r[2], 2, 1)
+        multiply(2, 1, (0, 1, 2), 2, 1)
+        grp_r[3] = regroup_on_tensor(raw_x[3][1], ("bank1", "bank0"))
+        unit(2, 0, ((0, 256, "scalar"), (256, 512, "gpsimd")), False)
+        sign(3, 0)
+        grp_r[0] = regroup_on_tensor(raw_x[0][1], ("bank1", "bank0"))
+        acc[3][1] = psum.tile([P, HALF], F32, name="acc31", tag="bank%d" % RIGHT_BANKS[3])
+        quantise_x(grp_r[3], 3, 1)
+        multiply(3, 1, (0, 1, 2), 2, 1)
+        unit(3, 0, ((0, 256, "scalar"), (256, 512, "gpsimd")), True)
+        grp_r[1] = regroup(raw_x[1][1], both)
         sign(0, 1)
         sign(1, 1)
-        unit(2, 0, (0, 512), (0, 256, 512), False)
+        quantise_x(grp_r[0], 0, 1)
+        multiply(0, 1, (0, 1, 2), 2, 1)
         quantise_x(grp_r[1], 1, 1)
-        grp_r.append(regroup(raw_x[3][1], 0))
+        multiply(1, 1, (0, 1, 2), 2, 1)
+        for c in (2, 3, 0, 1):
+            multiply(c, 1, (3,), 2, 1)
+        unit(0, 1, ((0, 256, "scalar"), (256, 512, "gpsimd")), False)
         sign(2, 1)
+        unit(1, 1, ((0, 256, "scalar"), (256, 512, "gpsimd")), True)
         sign(3, 1)
-        quantise_x(grp_r[2], 2, 1)
-        unit(3, 0, (0, 512), (0, 256, 512), True)
-        quantise_x(grp_r[3], 3, 1)
-        for ot in range(O_TILES):
-            unit(ot, 1, (0, 512), (0, 256, 512), True)
+        unit(2, 1, ((0, 256, "scalar"), (256, 512, "gpsimd")), True)
+        unit(3, 1, ((0, 256, "scalar"), (256, 512, "gpsimd")), True)

@@ -259,38 +259,39 @@ def tile_bitlinear_kernel(
             if kind == "x" and c < 2:
                 multiply(c, 0, range(O_TILES), 0, PASSES - 1)
 
-        for i, (kind, c) in enumerate(HEAD):
-            prepare(kind, c)
-            if i > 0:
-                finish()
-        last = PASSES - 1
-        grp_g = [None, None]
-        grp_g[0] = regroup(raw_g[2], ((vector_copy, 0, 128), (scalar_copy, 128, HALF)))
-        finish()
-        quantise_g(grp_g[0], 2, 0, 128)
-        multiply(2, 0, (0,), 0, last)
-        sign(0, 0)
-        grp_g[1] = regroup(raw_g[3], ((vector_copy, 0, 128), (scalar_copy, 256, 384)))
-        quantise_g(grp_g[1], 3, 0, 128)
-        multiply(3, 0, (0,), 0, last)
-        interleave(vector_copy, grp_g[1], raw_g[3], 128, 256)
-        quantise_g(grp_g[0], 2, 128, 256)
-        gs = gsp.tile([P, HALF], F32, name="gs")
-        scaled(gs, 0, 0, 0, 64)
-        quantise_g(grp_g[1], 3, 128, 256)
-        multiply(2, 0, (1,), 0, last)
-        multiply(3, 0, (1,), 0, last)
-        piece_of(gs, 0, 0, 0, 64, "scalar")
-        scaled(gs, 0, 0, 64, 256)
-        piece_of(gs, 0, 0, 64, 128, "scalar")
-        piece_of(gs, 0, 0, 128, 256, "scalar")
-        sign(1, 0)
-        scaled(gs, 0, 0, 256, 512)
-        piece_of(gs, 0, 0, 256, 512, "scalar")
-        unit(1, 0, ((0, 256, "scalar"), (256, 512, "gpsimd")), False)
+        with tc.manual_schedule():
+            for i, (kind, c) in enumerate(HEAD):
+                prepare(kind, c)
+                if i > 0:
+                    finish()
+            last = PASSES - 1
+            grp_g = [None, None]
+            grp_g[0] = regroup(raw_g[2], ((vector_copy, 0, 128), (scalar_copy, 128, HALF)))
+            finish()
+            quantise_g(grp_g[0], 2, 0, 128)
+            multiply(2, 0, (0,), 0, last)
+            sign(0, 0)
+            grp_g[1] = regroup(raw_g[3], ((vector_copy, 0, 128), (scalar_copy, 256, 384)))
+            quantise_g(grp_g[1], 3, 0, 128)
+            multiply(3, 0, (0,), 0, last)
+            interleave(vector_copy, grp_g[1], raw_g[3], 128, 256)
+            quantise_g(grp_g[0], 2, 128, 256)
+            gs = gsp.tile([P, HALF], F32, name="gs")
+            scaled(gs, 0, 0, 0, 64)
+            quantise_g(grp_g[1], 3, 128, 256)
+            multiply(2, 0, (1,), 0, last)
+            multiply(3, 0, (1,), 0, last)
+            piece_of(gs, 0, 0, 0, 64, "scalar")
+            scaled(gs, 0, 0, 64, 256)
+            piece_of(gs, 0, 0, 64, 128, "scalar")
+            piece_of(gs, 0, 0, 128, 256, "scalar")
+            sign(1, 0)
+            scaled(gs, 0, 0, 256, 512)
+            piece_of(gs, 0, 0, 256, 512, "scalar")
+            unit(1, 0, ((0, 256, "scalar"), (256, 512, "scalar")), False)
         interleave(scalar_copy, grp_g[1], raw_g[3], 384, HALF)
         grp_r = [None] * PASSES
-        grp_r[2] = regroup_on_tensor(raw_x[2][1], ("bank7", "bank0"))
+        grp_r[2] = regroup(raw_x[2][1], ((vector_copy, 0, 128),) + tuple((scalar_copy, lo, lo + 128) for lo in range(128, HALF, 128)))
         sign(2, 0)
         for c in (2, 3):
             quantise_g(grp_g[c - 2], c, 256, 512)
@@ -301,15 +302,15 @@ def tile_bitlinear_kernel(
             acc[ot][1] = psum.tile([P, HALF], F32, name="acc%d1" % ot, tag="bank%d" % RIGHT_BANKS[ot])
         quantise_x(grp_r[2], 2, 1)
         multiply(2, 1, (0, 1, 2), 2, 1)
-        grp_r[3] = regroup_on_tensor(raw_x[3][1], ("bank1", "bank0"))
+        grp_r[3] = regroup(raw_x[3][1], ((vector_copy, 0, 128),) + tuple((scalar_copy, lo, lo + 128) for lo in range(128, HALF, 128)))
         unit(2, 0, ((0, 256, "scalar"), (256, 512, "gpsimd")), False)
         sign(3, 0)
-        grp_r[0] = regroup_on_tensor(raw_x[0][1], ("bank1", "bank0"))
+        grp_r[0] = regroup(raw_x[0][1], ((vector_copy, 0, 128),) + tuple((scalar_copy, lo, lo + 128) for lo in range(128, HALF, 128)))
         acc[3][1] = psum.tile([P, HALF], F32, name="acc31", tag="bank%d" % RIGHT_BANKS[3])
         quantise_x(grp_r[3], 3, 1)
         multiply(3, 1, (0, 1, 2), 2, 1)
         unit(3, 0, ((0, 256, "scalar"), (256, 512, "gpsimd")), True)
-        grp_r[1] = regroup(raw_x[1][1], both)
+        grp_r[1] = regroup(raw_x[1][1], ((vector_copy, 0, 128),) + tuple((scalar_copy, lo, lo + 128) for lo in range(128, HALF, 128)))
         sign(0, 1)
         sign(1, 1)
         quantise_x(grp_r[0], 0, 1)

@@ -42,11 +42,12 @@ def tile_bitlinear_kernel(
     with ExitStack() as ctx:
         keep = ctx.enter_context(tc.tile_pool(name="keep", bufs=1))
         rawp = ctx.enter_context(tc.tile_pool(name="rawp", bufs=1))
-        grpp = ctx.enter_context(tc.tile_pool(name="grpp", bufs=4))
-        gsp = ctx.enter_context(tc.tile_pool(name="gsp", bufs=3))
+        grpp = ctx.enter_context(tc.tile_pool(name="grpp", bufs=6))
+        gsp = ctx.enter_context(tc.tile_pool(name="gsp", bufs=4))
         hp = ctx.enter_context(tc.tile_pool(name="hp", bufs=6))
-        bigp = ctx.enter_context(tc.tile_pool(name="bigp", bufs=4))
+        wholep = ctx.enter_context(tc.tile_pool(name="wholep", bufs=3))
         psum = ctx.enter_context(tc.psum_pool(name="psum", bufs=1))
+        ctx.enter_context(tc.manual_schedule())
 
         warm = keep.tile([P, 1], F32, name="warm")
         sc_bf = keep.tile([P, 1], BF16, name="sc_bf")
@@ -120,24 +121,27 @@ def tile_bitlinear_kernel(
                 interleave(copy, grp, raw, lo, hi)
             return grp
 
-        def regroup_on_tensor(raw, banks):
-            grp = grpp.tile([P, HALF, PACK], BF16, name="grp", align_bytes=64)
-            for part, bank in enumerate(banks):
-                turned = psum.tile([P, 2 * HALF], BF16, name="turned", tag=bank)
-                for q in range(2):
-                    lo = part * 256 + q * P
-                    nc.tensor.matmul(
-                        out=turned[:, q * HALF : (q + 1) * HALF],
-                        lhsT=ident[:],
-                        rhs=raw[:, :, lo : lo + P].rearrange("p t c -> p c t"),
-                        start=True,
-                        stop=True,
-                    )
-                nc.scalar.copy(
-                    out=grp[:, part * 256 : (part + 1) * 256, :].rearrange("p w t -> p (w t)"),
-                    in_=turned[:],
+        def new_grp():
+            return grpp.tile([P, HALF, PACK], BF16, name="grp", align_bytes=64)
+
+        def turn(raw, part, bank):
+            turned = psum.tile([P, 2 * HALF], BF16, name="turned", tag=bank)
+            for q in range(2):
+                lo = part * 256 + q * P
+                nc.tensor.matmul(
+                    out=turned[:, q * HALF : (q + 1) * HALF],
+                    lhsT=ident[:],
+                    rhs=raw[:, :, lo : lo + P].rearrange("p t c -> p c t"),
+                    start=True,
+                    stop=True,
                 )
-            return grp
+            return turned
+
+        def collect(turned, grp, part):
+            nc.scalar.copy(
+                out=grp[:, part * 256 : (part + 1) * 256, :].rearrange("p w t -> p (w t)"),
+                in_=turned[:],
+            )
 
         def quantise_g(grp, c, lo, hi):
             nc.vector.quantize_mx(
@@ -210,35 +214,29 @@ def tile_bitlinear_kernel(
                 out=out[ot * P : (ot + 1) * P, h * HALF + lo : h * HALF + hi, :], in_=planes
             )
 
-        def piece_of(gs, ot, h, lo, hi, where):
-            piece = hp.tile([P, hi - lo, NBITS], F32, name="piece")
-            expand(piece[:], gs, lo, hi, 4)
-            low_planes(piece[:], where == "gpsimd")
-            store(piece[:], ot, h, lo, hi)
-
-        def unit(ot, h, pieces, one_store, gs_cuts=(0, HALF)):
+        def new_gs(ot, h, lo=0, hi=HALF):
             gs = gsp.tile([P, HALF], F32, name="gs")
-            if one_store:
-                whole = bigp.tile([P, HALF, NBITS], F32, name="whole")
-            n = 0
-            for lo, hi, where in pieces:
-                while gs_cuts[n] < hi:
-                    scaled(gs, ot, h, gs_cuts[n], gs_cuts[n + 1])
-                    n += 1
-                if one_store:
-                    planes = whole[:, lo:hi, :]
-                else:
-                    piece = hp.tile([P, hi - lo, NBITS], F32, name="piece")
-                    planes = piece[:]
-                if where == "vector":
-                    expand(planes, gs, lo, hi, NBITS)
-                else:
-                    expand(planes, gs, lo, hi, 4)
-                    low_planes(planes, where == "gpsimd")
-                if not one_store:
-                    store(planes, ot, h, lo, hi)
-            if one_store:
-                store(whole[:], ot, h, 0, HALF)
+            scaled(gs, ot, h, lo, hi)
+            return gs
+
+        S, G, SG = (False,), (True,), (False, True)
+
+        def piece(gs, ot, h, lo, hi, lows):
+            tile = hp.tile([P, hi - lo, NBITS], F32, name="piece")
+            share = (hi - lo) // len(lows)
+            for k, on_gpsimd in enumerate(lows):
+                part = tile[:, k * share : (k + 1) * share, :]
+                expand(part, gs, lo + k * share, lo + (k + 1) * share, 4)
+                low_planes(part, on_gpsimd)
+            store(tile[:], ot, h, lo, hi)
+
+        def half_of(big, gs, lo, low):
+            expand(big[:, lo : lo + 256, :], gs, lo, lo + 256, 4)
+            low_planes(big[:, lo : lo + 256, :], low[0])
+
+        def halves(big, gs, lows):
+            half_of(big, gs, 0, lows[0])
+            half_of(big, gs, 256, lows[1])
 
         vector_copy = nc.vector.tensor_copy
         scalar_copy = nc.scalar.copy
@@ -259,69 +257,88 @@ def tile_bitlinear_kernel(
             if kind == "x" and c < 2:
                 multiply(c, 0, range(O_TILES), 0, PASSES - 1)
 
-        with tc.manual_schedule():
-            for i, (kind, c) in enumerate(HEAD):
-                prepare(kind, c)
-                if i > 0:
-                    finish()
-            last = PASSES - 1
-            grp_g = [None, None]
-            grp_g[0] = regroup(raw_g[2], ((vector_copy, 0, 128), (scalar_copy, 128, HALF)))
-            finish()
-            quantise_g(grp_g[0], 2, 0, 128)
-            multiply(2, 0, (0,), 0, last)
-            sign(0, 0)
-            grp_g[1] = regroup(raw_g[3], ((vector_copy, 0, 128), (scalar_copy, 256, 384)))
-            quantise_g(grp_g[1], 3, 0, 128)
-            multiply(3, 0, (0,), 0, last)
-            interleave(vector_copy, grp_g[1], raw_g[3], 128, 256)
-            quantise_g(grp_g[0], 2, 128, 256)
-            gs = gsp.tile([P, HALF], F32, name="gs")
-            scaled(gs, 0, 0, 0, 64)
-            quantise_g(grp_g[1], 3, 128, 256)
-            multiply(2, 0, (1,), 0, last)
-            multiply(3, 0, (1,), 0, last)
-            piece_of(gs, 0, 0, 0, 64, "scalar")
-            scaled(gs, 0, 0, 64, 256)
-            piece_of(gs, 0, 0, 64, 128, "scalar")
-            piece_of(gs, 0, 0, 128, 256, "scalar")
-            sign(1, 0)
-            scaled(gs, 0, 0, 256, 512)
-            piece_of(gs, 0, 0, 256, 512, "scalar")
-            unit(1, 0, ((0, 256, "scalar"), (256, 512, "scalar")), False)
-        interleave(scalar_copy, grp_g[1], raw_g[3], 384, HALF)
-        grp_r = [None] * PASSES
-        grp_r[2] = regroup(raw_x[2][1], ((vector_copy, 0, 128),) + tuple((scalar_copy, lo, lo + 128) for lo in range(128, HALF, 128)))
-        sign(2, 0)
+        for i, (kind, c) in enumerate(HEAD):
+            prepare(kind, c)
+            if i > 0:
+                finish()
+        last = PASSES - 1
+        every = range(O_TILES)
+        grp_g = [None, None]
+        grp_g[0] = regroup(raw_g[2], ((vector_copy, 0, 128), (scalar_copy, 128, HALF)))
+        finish()
+        quantise_g(grp_g[0], 2, 0, 128)
+        multiply(2, 0, (0,), 0, last)
+        sign(0, 0)
+        grp_g[1] = regroup(raw_g[3], ((vector_copy, 0, 128), (scalar_copy, 256, HALF)))
+        quantise_g(grp_g[1], 3, 0, 128)
+        multiply(3, 0, (0,), 0, last)
+        interleave(vector_copy, grp_g[1], raw_g[3], 128, 256)
+        quantise_g(grp_g[0], 2, 128, 256)
+        gs0 = new_gs(0, 0, 0, 64)
+        quantise_g(grp_g[1], 3, 128, 256)
+        for c in (2, 3):
+            multiply(c, 0, (1,), 0, last)
+        piece(gs0, 0, 0, 0, 64, S)
+        scaled(gs0, 0, 0, 64, 256)
+        piece(gs0, 0, 0, 64, 128, S)
+        piece(gs0, 0, 0, 128, 256, S)
+        sign(1, 0)
+        scaled(gs0, 0, 0, 256, 512)
+        grp_r = [new_grp() for c in range(PASSES)]
+        turned = [turn(raw_x[3][1], 0, "bank7"), turn(raw_x[3][1], 1, "bank5")]
+        piece(gs0, 0, 0, 256, 512, S + S)
         for c in (2, 3):
             quantise_g(grp_g[c - 2], c, 256, 512)
         for ot in (2, 3):
             for c in (2, 3):
                 multiply(c, 0, (ot,), 0, last)
+        gs1 = new_gs(1, 0)
+        collect(turned[0], grp_r[3], 0)
+        piece(gs1, 1, 0, 0, 256, SG)
+        sign(2, 0)
+        collect(turned[1], grp_r[3], 1)
+        turned = [turn(raw_x[0][1], 0, "bank6"), turn(raw_x[0][1], 1, "bank1")]
+        sign(3, 0)
+        piece(gs1, 1, 0, 256, 512, G)
+        gs2 = new_gs(2, 0)
+        collect(turned[0], grp_r[0], 0)
+        collect(turned[1], grp_r[0], 1)
+        turned = [turn(raw_x[2][1], 0, "bank7"), turn(raw_x[2][1], 1, "bank5")]
+        piece(gs2, 2, 0, 0, 256, S)
+        interleave(scalar_copy, grp_r[1], raw_x[1][1], 256, 512)
+        gs3 = new_gs(3, 0)
+        piece(gs2, 2, 0, 256, 512, G)
+        collect(turned[0], grp_r[2], 0)
+        collect(turned[1], grp_r[2], 1)
+        sign(0, 1)
         for ot in range(O_TILES - 1):
             acc[ot][1] = psum.tile([P, HALF], F32, name="acc%d1" % ot, tag="bank%d" % RIGHT_BANKS[ot])
-        quantise_x(grp_r[2], 2, 1)
-        multiply(2, 1, (0, 1, 2), 2, 1)
-        grp_r[3] = regroup(raw_x[3][1], ((vector_copy, 0, 128),) + tuple((scalar_copy, lo, lo + 128) for lo in range(128, HALF, 128)))
-        unit(2, 0, ((0, 256, "scalar"), (256, 512, "gpsimd")), False)
-        sign(3, 0)
-        grp_r[0] = regroup(raw_x[0][1], ((vector_copy, 0, 128),) + tuple((scalar_copy, lo, lo + 128) for lo in range(128, HALF, 128)))
         acc[3][1] = psum.tile([P, HALF], F32, name="acc31", tag="bank%d" % RIGHT_BANKS[3])
-        quantise_x(grp_r[3], 3, 1)
-        multiply(3, 1, (0, 1, 2), 2, 1)
-        unit(3, 0, ((0, 256, "scalar"), (256, 512, "gpsimd")), True)
-        grp_r[1] = regroup(raw_x[1][1], ((vector_copy, 0, 128),) + tuple((scalar_copy, lo, lo + 128) for lo in range(128, HALF, 128)))
-        sign(0, 1)
+        whole = wholep.tile([P, HALF, NBITS], F32, name="whole")
+        half_of(whole[:], gs3, 0, S)
+        half_of(whole[:], gs3, 256, S)
+        store(whole[:], 3, 0, 0, HALF)
+        interleave(vector_copy, grp_r[1], raw_x[1][1], 0, 256)
+        for c in (3, 0, 1, 2):
+            quantise_x(grp_r[c], c, 1)
+        for ot in every:
+            for c in (3, 0, 1, 2):
+                multiply(c, 1, (ot,), 3, 2)
         sign(1, 1)
-        quantise_x(grp_r[0], 0, 1)
-        multiply(0, 1, (0, 1, 2), 2, 1)
-        quantise_x(grp_r[1], 1, 1)
-        multiply(1, 1, (0, 1, 2), 2, 1)
-        for c in (2, 3, 0, 1):
-            multiply(c, 1, (3,), 2, 1)
-        unit(0, 1, ((0, 256, "scalar"), (256, 512, "gpsimd")), False)
+        gs0 = new_gs(0, 1)
+        piece(gs0, 0, 1, 0, 256, S)
+        gs1 = new_gs(1, 1)
+        piece(gs0, 0, 1, 256, 512, SG)
         sign(2, 1)
-        unit(1, 1, ((0, 256, "scalar"), (256, 512, "gpsimd")), True)
         sign(3, 1)
-        unit(2, 1, ((0, 256, "scalar"), (256, 512, "gpsimd")), True)
-        unit(3, 1, ((0, 256, "scalar"), (256, 512, "gpsimd")), True)
+        whole = wholep.tile([P, HALF, NBITS], F32, name="whole")
+        halves(whole[:], gs1, (S, G))
+        store(whole[:], 1, 1, 0, HALF)
+        gs2 = new_gs(2, 1)
+        whole = wholep.tile([P, HALF, NBITS], F32, name="whole")
+        halves(whole[:], gs2, (S, G))
+        store(whole[:], 2, 1, 0, HALF)
+        gs3 = new_gs(3, 1)
+        whole = wholep.tile([P, HALF, NBITS], F32, name="whole")
+        halves(whole[:], gs3, (S, G))
+        store(whole[:], 3, 1, 0, HALF)

@@ -230,6 +230,14 @@ def tile_bitlinear_kernel(
                 low_planes(part, on_gpsimd)
             store(tile[:], ot, h, lo, hi)
 
+        def new_piece(width):
+            return hp.tile([P, width, NBITS], F32, name="piece")
+
+        def part(tile, gs, base, lo, hi, low):
+            planes = tile[:, lo - base : hi - base, :]
+            expand(planes, gs, lo, hi, 4)
+            low_planes(planes, low[0])
+
         def half_of(big, gs, lo, low):
             expand(big[:, lo : lo + 256, :], gs, lo, lo + 256, 4)
             low_planes(big[:, lo : lo + 256, :], low[0])
@@ -279,28 +287,31 @@ def tile_bitlinear_kernel(
         for c in (2, 3):
             multiply(c, 0, (1,), 0, last)
         piece(gs0, 0, 0, 0, 64, S)
+        sign(1, 0)
         scaled(gs0, 0, 0, 64, 256)
+        scaled(gs0, 0, 0, 256, 512)
         piece(gs0, 0, 0, 64, 128, S)
         piece(gs0, 0, 0, 128, 256, S)
-        sign(1, 0)
-        scaled(gs0, 0, 0, 256, 512)
         grp_r = [new_grp() for c in range(PASSES)]
         turned = [turn(raw_x[3][1], 0, "bank7"), turn(raw_x[3][1], 1, "bank5")]
-        piece(gs0, 0, 0, 256, 512, S + S)
+        tile = new_piece(256)
+        part(tile, gs0, 256, 256, 384, S)
+        part(tile, gs0, 256, 384, 512, S)
+        store(tile[:], 0, 0, 256, 512)
+        sign(2, 0)
+        gs1 = new_gs(1, 0)
         for c in (2, 3):
             quantise_g(grp_g[c - 2], c, 256, 512)
         for ot in (2, 3):
             for c in (2, 3):
                 multiply(c, 0, (ot,), 0, last)
-        gs1 = new_gs(1, 0)
         collect(turned[0], grp_r[3], 0)
         piece(gs1, 1, 0, 0, 256, SG)
-        sign(2, 0)
         collect(turned[1], grp_r[3], 1)
         turned = [turn(raw_x[0][1], 0, "bank6"), turn(raw_x[0][1], 1, "bank1")]
-        sign(3, 0)
-        piece(gs1, 1, 0, 256, 512, G)
         gs2 = new_gs(2, 0)
+        piece(gs1, 1, 0, 256, 512, G)
+        sign(3, 0)
         collect(turned[0], grp_r[0], 0)
         collect(turned[1], grp_r[0], 1)
         turned = [turn(raw_x[2][1], 0, "bank7"), turn(raw_x[2][1], 1, "bank5")]
@@ -310,14 +321,14 @@ def tile_bitlinear_kernel(
         piece(gs2, 2, 0, 256, 512, G)
         collect(turned[0], grp_r[2], 0)
         collect(turned[1], grp_r[2], 1)
-        sign(0, 1)
-        for ot in range(O_TILES - 1):
-            acc[ot][1] = psum.tile([P, HALF], F32, name="acc%d1" % ot, tag="bank%d" % RIGHT_BANKS[ot])
-        acc[3][1] = psum.tile([P, HALF], F32, name="acc31", tag="bank%d" % RIGHT_BANKS[3])
+        for ot in range(O_TILES):
+            bank = psum.tile([P, HALF], F32, name="acc%d1" % ot, tag="bank%d" % RIGHT_BANKS[ot])
+            acc[ot][1] = bank
         whole = wholep.tile([P, HALF, NBITS], F32, name="whole")
         half_of(whole[:], gs3, 0, S)
         half_of(whole[:], gs3, 256, S)
         store(whole[:], 3, 0, 0, HALF)
+        sign(0, 1)
         interleave(vector_copy, grp_r[1], raw_x[1][1], 0, 256)
         for c in (3, 0, 1, 2):
             quantise_x(grp_r[c], c, 1)
@@ -332,13 +343,15 @@ def tile_bitlinear_kernel(
         sign(2, 1)
         sign(3, 1)
         whole = wholep.tile([P, HALF, NBITS], F32, name="whole")
-        halves(whole[:], gs1, (S, G))
-        store(whole[:], 1, 1, 0, HALF)
+        half_of(whole[:], gs1, 0, S)
         gs2 = new_gs(2, 1)
+        half_of(whole[:], gs1, 256, G)
+        store(whole[:], 1, 1, 0, HALF)
         whole = wholep.tile([P, HALF, NBITS], F32, name="whole")
-        halves(whole[:], gs2, (S, G))
-        store(whole[:], 2, 1, 0, HALF)
+        half_of(whole[:], gs2, 0, S)
         gs3 = new_gs(3, 1)
+        half_of(whole[:], gs2, 256, G)
+        store(whole[:], 2, 1, 0, HALF)
         whole = wholep.tile([P, HALF, NBITS], F32, name="whole")
         halves(whole[:], gs3, (S, G))
         store(whole[:], 3, 1, 0, HALF)

@@ -38,14 +38,17 @@ def tile_bitlinear_kernel(
     x2 = x.rearrange("b s i -> (b s) i")
     g2 = grad_out.rearrange("b s o -> (b s) o")
     ws_view = wsign.rearrange("(t p) i -> p t i", p=P)
+    out_view = out.rearrange("(t p) i j -> p t i j", p=P)
 
     with ExitStack() as ctx:
         keep = ctx.enter_context(tc.tile_pool(name="keep", bufs=1))
         rawp = ctx.enter_context(tc.tile_pool(name="rawp", bufs=1))
-        grpp = ctx.enter_context(tc.tile_pool(name="grpp", bufs=6))
+        grpp = ctx.enter_context(tc.tile_pool(name="grpp", bufs=5))
         gsp = ctx.enter_context(tc.tile_pool(name="gsp", bufs=4))
-        hp = ctx.enter_context(tc.tile_pool(name="hp", bufs=6))
+        smallp = ctx.enter_context(tc.tile_pool(name="smallp", bufs=3))
+        hp = ctx.enter_context(tc.tile_pool(name="hp", bufs=3))
         wholep = ctx.enter_context(tc.tile_pool(name="wholep", bufs=3))
+        bigp = ctx.enter_context(tc.tile_pool(name="bigp", bufs=1))
         psum = ctx.enter_context(tc.psum_pool(name="psum", bufs=1))
         ctx.enter_context(tc.manual_schedule())
 
@@ -222,7 +225,7 @@ def tile_bitlinear_kernel(
         S, G, SG = (False,), (True,), (False, True)
 
         def piece(gs, ot, h, lo, hi, lows):
-            tile = hp.tile([P, hi - lo, NBITS], F32, name="piece")
+            tile = smallp.tile([P, hi - lo, NBITS], F32, name="small")
             share = (hi - lo) // len(lows)
             for k, on_gpsimd in enumerate(lows):
                 part = tile[:, k * share : (k + 1) * share, :]
@@ -238,6 +241,15 @@ def tile_bitlinear_kernel(
             expand(planes, gs, lo, hi, 4)
             low_planes(planes, low[0])
 
+        def on_gpsimd(planes, gs, lo, hi):
+            nc.gpsimd.tensor_tensor(
+                out=planes[:, :, 0:4],
+                in0=gs[:, lo:hi].unsqueeze(2).to_broadcast([P, hi - lo, 4]),
+                in1=e_sb[:].unsqueeze(1).to_broadcast([P, hi - lo, 4]),
+                op=MULT,
+            )
+            low_planes(planes, True)
+
         def half_of(big, gs, lo, low):
             expand(big[:, lo : lo + 256, :], gs, lo, lo + 256, 4)
             low_planes(big[:, lo : lo + 256, :], low[0])
@@ -248,6 +260,8 @@ def tile_bitlinear_kernel(
 
         vector_copy = nc.vector.tensor_copy
         scalar_copy = nc.scalar.copy
+        e_sb = keep.tile([P, 4], F32, name="e_sb")
+        nc.vector.tensor_copy(out=e_sb[:], in_=e8[:, 0:4])
         both = ((vector_copy, 0, 256), (scalar_copy, 256, HALF))
 
         pending = []
@@ -305,29 +319,38 @@ def tile_bitlinear_kernel(
         for ot in (2, 3):
             for c in (2, 3):
                 multiply(c, 0, (ot,), 0, last)
+        tile_a = new_piece(256)
+        tile_b = new_piece(256)
+        on_gpsimd(tile_b[:, 128:256, :], gs1, 384, 512)
         collect(turned[0], grp_r[3], 0)
-        piece(gs1, 1, 0, 0, 256, SG)
+        part(tile_a, gs1, 0, 0, 128, S)
+        part(tile_a, gs1, 0, 128, 256, S)
+        store(tile_a[:], 1, 0, 0, 256)
+        sign(3, 0)
+        gs2 = new_gs(2, 0)
+        part(tile_b, gs1, 256, 256, 384, S)
+        store(tile_b[:], 1, 0, 256, 512)
         collect(turned[1], grp_r[3], 1)
         turned = [turn(raw_x[0][1], 0, "bank6"), turn(raw_x[0][1], 1, "bank1")]
-        gs2 = new_gs(2, 0)
-        piece(gs1, 1, 0, 256, 512, G)
-        sign(3, 0)
+        whole2 = wholep.tile([P, HALF, NBITS], F32, name="whole")
+        on_gpsimd(whole2[:, 384:512, :], gs2, 384, 512)
+        part(whole2, gs2, 0, 0, 256, S)
+        gs3 = new_gs(3, 0)
+        part(whole2, gs2, 0, 256, 384, G)
+        store(whole2[:], 2, 0, 0, HALF)
         collect(turned[0], grp_r[0], 0)
         collect(turned[1], grp_r[0], 1)
         turned = [turn(raw_x[2][1], 0, "bank7"), turn(raw_x[2][1], 1, "bank5")]
-        piece(gs2, 2, 0, 0, 256, S)
         interleave(scalar_copy, grp_r[1], raw_x[1][1], 256, 512)
-        gs3 = new_gs(3, 0)
-        piece(gs2, 2, 0, 256, 512, G)
+        whole3 = wholep.tile([P, HALF, NBITS], F32, name="whole")
+        half_of(whole3[:], gs3, 0, S)
         collect(turned[0], grp_r[2], 0)
         collect(turned[1], grp_r[2], 1)
         for ot in range(O_TILES):
             bank = psum.tile([P, HALF], F32, name="acc%d1" % ot, tag="bank%d" % RIGHT_BANKS[ot])
             acc[ot][1] = bank
-        whole = wholep.tile([P, HALF, NBITS], F32, name="whole")
-        half_of(whole[:], gs3, 0, S)
-        half_of(whole[:], gs3, 256, S)
-        store(whole[:], 3, 0, 0, HALF)
+        half_of(whole3[:], gs3, 256, S)
+        store(whole3[:], 3, 0, 0, HALF)
         sign(0, 1)
         interleave(vector_copy, grp_r[1], raw_x[1][1], 0, 256)
         for c in (3, 0, 1, 2):
@@ -336,22 +359,27 @@ def tile_bitlinear_kernel(
             for c in (3, 0, 1, 2):
                 multiply(c, 1, (ot,), 3, 2)
         sign(1, 1)
-        gs0 = new_gs(0, 1)
-        piece(gs0, 0, 1, 0, 256, S)
-        gs1 = new_gs(1, 1)
-        piece(gs0, 0, 1, 256, 512, SG)
         sign(2, 1)
+        gs0 = new_gs(0, 1)
+        whole0 = wholep.tile([P, HALF, NBITS], F32, name="whole")
+        on_gpsimd(whole0[:, 384:512, :], gs0, 384, 512)
+        part(whole0, gs0, 0, 0, 256, S)
+        gs1 = new_gs(1, 1)
+        part(whole0, gs0, 0, 256, 384, S)
+        store(whole0[:], 0, 1, 0, HALF)
         sign(3, 1)
-        whole = wholep.tile([P, HALF, NBITS], F32, name="whole")
-        half_of(whole[:], gs1, 0, S)
+        whole1 = wholep.tile([P, HALF, NBITS], F32, name="whole")
+        on_gpsimd(whole1[:, 384:512, :], gs1, 384, 512)
+        part(whole1, gs1, 0, 0, 256, S)
         gs2 = new_gs(2, 1)
-        half_of(whole[:], gs1, 256, G)
-        store(whole[:], 1, 1, 0, HALF)
-        whole = wholep.tile([P, HALF, NBITS], F32, name="whole")
-        half_of(whole[:], gs2, 0, S)
+        part(whole1, gs1, 0, 256, 384, S)
+        store(whole1[:], 1, 1, 0, HALF)
+        pair = bigp.tile([P, 2, HALF, NBITS], F32, name="pair")
+        on_gpsimd(pair[:, 0, 384:512, :], gs2, 384, 512)
+        part(pair[:, 0, :, :], gs2, 0, 0, 256, S)
         gs3 = new_gs(3, 1)
-        half_of(whole[:], gs2, 256, G)
-        store(whole[:], 2, 1, 0, HALF)
-        whole = wholep.tile([P, HALF, NBITS], F32, name="whole")
-        halves(whole[:], gs3, (S, G))
-        store(whole[:], 3, 1, 0, HALF)
+        part(pair[:, 0, :, :], gs2, 0, 256, 384, S)
+        on_gpsimd(pair[:, 1, 384:512, :], gs3, 384, 512)
+        part(pair[:, 1, :, :], gs3, 0, 0, 256, S)
+        part(pair[:, 1, :, :], gs3, 0, 256, 384, S)
+        nc.sync.dma_start(out=out_view[:, 2:4, HALF:IN, :], in_=pair[:])

@@ -313,12 +313,12 @@ def tile_bitlinear_kernel(
         part(tile, gs0, 256, 384, 512, S)
         store(tile[:], 0, 0, 256, 512)
         sign(2, 0)
-        gs1 = new_gs(1, 0)
         for c in (2, 3):
             quantise_g(grp_g[c - 2], c, 256, 512)
         for ot in (2, 3):
             for c in (2, 3):
                 multiply(c, 0, (ot,), 0, last)
+        gs1 = new_gs(1, 0)
         tile_a = new_piece(256)
         tile_b = new_piece(256)
         on_gpsimd(tile_b[:, 128:256, :], gs1, 384, 512)

from contextlib import ExitStack

import concourse.mybir as mybir
from concourse.masks import make_identity

BF16 = mybir.dt.bfloat16
F32 = mybir.dt.float32
U32 = mybir.dt.uint32
U8 = mybir.dt.uint8
E4M3X4 = mybir.dt.float8_e4m3fn_x4
E5M2X4 = mybir.dt.float8_e5m2_x4
MULT = mybir.AluOpType.mult
ACT = mybir.ActivationFunctionType

P = 128
PACK = 4
K_PASS = P * PACK
T = 2048
IN = 1024
OUT = 512
NBITS = 8
PASSES = T // K_PASS
HALF = 512
O_TILES = OUT // P
RUN = 4
HEAD = (("g", 0), ("x", 0), ("g", 1), ("x", 1), ("x", 2), ("x", 3))
RIGHT_BANKS = (5, 6, 7, 0)
WHOLE = 3

FLOPS = 2 * T * IN * OUT
BYTES = 2 * (T * IN + T * OUT + OUT * IN + 1) + 4 * OUT * IN * NBITS


def tile_bitlinear_kernel(
    tc, x, bweight, wsign, scale, bbias, bsign, biasscale, grad_out, out
):
    nc = tc.nc
    x2 = x.rearrange("b s i -> (b s) i")
    g2 = grad_out.rearrange("b s o -> (b s) o")
    ws_view = wsign.rearrange("(t p) i -> p t i", p=P)
    out_view = out.rearrange("(t p) i j -> p t i j", p=P)

    with ExitStack() as ctx:
        keep = ctx.enter_context(tc.tile_pool(name="keep", bufs=1))
        rawp = ctx.enter_context(tc.tile_pool(name="rawp", bufs=1))
        grpp = ctx.enter_context(tc.tile_pool(name="grpp", bufs=5))
        gsp = ctx.enter_context(tc.tile_pool(name="gsp", bufs=4))
        smallp = ctx.enter_context(tc.tile_pool(name="smallp", bufs=3))
        hp = ctx.enter_context(tc.tile_pool(name="hp", bufs=3))
        wholep = ctx.enter_context(tc.tile_pool(name="wholep", bufs=3))
        bigp = ctx.enter_context(tc.tile_pool(name="bigp", bufs=1))
        psum = ctx.enter_context(tc.psum_pool(name="psum", bufs=1))
        ctx.enter_context(tc.manual_schedule())

        warm = keep.tile([P, 1], F32, name="warm")
        sc_bf = keep.tile([P, 1], BF16, name="sc_bf")
        pw = keep.tile([P, NBITS], BF16, name="pw")
        ws = keep.tile([P, O_TILES, IN], BF16, name="ws")
        sgn = keep.tile([P, O_TILES, IN], BF16, name="sgn")
        g_codes = keep.tile([P, PASSES, OUT], U32, name="g_codes", align_bytes=64)
        g_scales = keep.tile([P, PASSES, OUT], U8, name="g_scales", align_bytes=64)
        x_codes = keep.tile([P, PASSES, IN], U32, name="x_codes", align_bytes=64)
        x_scales = keep.tile([P, PASSES, IN], U8, name="x_scales", align_bytes=64)
        acc = [
            [psum.tile([P, HALF], F32, name="acc%d0" % ot, tag="bank%d" % ot), None]
            for ot in range(O_TILES)
        ]
        e8 = psum.tile([P, HALF], F32, name="e8", tag="bank4")
        ones = keep.tile([P, P], BF16, name="ones")
        table = keep.tile([P, 32], BF16, name="table")
        ident = keep.tile([P, P], BF16, name="ident")
        make_identity(nc, ident[:])

        nc.scalar.dma_start(out=sc_bf[0:1, 0:1], in_=scale.unsqueeze(0))
        nc.vector.memset(ones[:], 1.0)
        nc.vector.memset(table[:], 0.0)
        for j in range(NBITS):
            nc.vector.memset(pw[:, j : j + 1], 2.0 ** (7 - j))
        nc.vector.tensor_scalar(
            out=table[0:1, 0:NBITS], in0=pw[0:1, 0:NBITS], scalar1=sc_bf[0:1, 0:1], scalar2=None, op0=MULT
        )
        nc.tensor.matmul(out=e8[:, 0:32], lhsT=ones[:], rhs=table[:], start=True, stop=True)
        nc.scalar.activation(out=warm[:], in_=ones[:, 0:1], func=ACT.Sign)

        def load(name, rows, width):
            raw = rawp.tile([P, PACK, width], BF16, name=name)
            nc.sync.dma_start(out=raw[:], in_=rows.rearrange("(p j) w -> p j w", j=PACK))
            return raw

        def rows_of(c):
            return slice(c * K_PASS, (c + 1) * K_PASS)

        raw_g = [None] * PASSES
        raw_x = [[None, None] for c in range(PASSES)]

        def load_g(c):
            raw_g[c] = load("raw_g%d" % c, g2[rows_of(c), :], OUT)[:]

        def load_x(c):
            if c >= WHOLE:
                whole = load("raw_x%d" % c, x2[rows_of(c), :], IN)
                raw_x[c] = [whole[:, :, 0:HALF], whole[:, :, HALF:IN]]
            else:
                raw_x[c][0] = load("raw_xl%d" % c, x2[rows_of(c), 0:HALF], HALF)[:]

        for kind, c in HEAD:
            (load_g if kind == "g" else load_x)(c)
        load_g(2)
        load_g(3)
        nc.sync.dma_start(out=ws[:, 0:1, :], in_=ws_view[:, 0:1, :])
        nc.sync.dma_start(out=ws[:, 1:4, :], in_=ws_view[:, 1:4, :])
        for c in range(WHOLE):
            raw_x[c][1] = load("raw_xr%d" % c, x2[rows_of(c), HALF:IN], HALF)[:]

        def interleave(copy, grp, raw, lo, hi):
            copy(
                out=grp[:, lo:hi, :].rearrange("p (c i) t -> p c t i", i=RUN),
                in_=raw[:, :, lo:hi].rearrange("p t (c i) -> p c t i", i=RUN),
            )

        def regroup(raw, shares):
            grp = grpp.tile([P, HALF, PACK], BF16, name="grp", align_bytes=64)
            for copy, lo, hi in shares:
                interleave(copy, grp, raw, lo, hi)
            return grp

        def new_grp():
            return grpp.tile([P, HALF, PACK], BF16, name="grp", align_bytes=64)

        def turn(raw, part, bank):
            turned = psum.tile([P, 2 * HALF], BF16, name="turned", tag=bank)
            for q in range(2):
                lo = part * 256 + q * P
                nc.tensor.matmul(
                    out=turned[:, q * HALF : (q + 1) * HALF],
                    lhsT=ident[:],
                    rhs=raw[:, :, lo : lo + P].rearrange("p t c -> p c t"),
                    start=True,
                    stop=True,
                )
            return turned

        def collect(turned, grp, part):
            nc.scalar.copy(
                out=grp[:, part * 256 : (part + 1) * 256, :].rearrange("p w t -> p (w t)"),
                in_=turned[:],
            )

        def quantise_g(grp, c, lo, hi):
            nc.vector.quantize_mx(
                out=g_codes[:, c, lo:hi].bitcast(E5M2X4),
                scales=g_scales[:, c, lo:hi],
                in_=grp[:, lo:hi, :].rearrange("p w t -> p (w t)"),
            )

        def quantise_x(grp, c, h):
            cols = slice(h * HALF, (h + 1) * HALF)
            nc.vector.quantize_mx(
                out=x_codes[:, c, cols].bitcast(E4M3X4),
                scales=x_scales[:, c, cols],
                in_=grp[:].rearrange("p w t -> p (w t)"),
            )

        def multiply(c, h, o_tiles, first, last):
            cols = slice(h * HALF, (h + 1) * HALF)
            for ot in o_tiles:
                o_cols = slice(ot * P, (ot + 1) * P)
                nc.tensor.matmul_mx(
                    out=acc[ot][h][:],
                    lhsT=g_codes[:, c, o_cols].bitcast(E5M2X4),
                    lhsT_scale=g_scales[:, c, o_cols],
                    rhs=x_codes[:, c, cols].bitcast(E4M3X4),
                    rhs_scale=x_scales[:, c, cols],
                    start=(c == first),
                    stop=(c == last),
                )

        def sign(ot, h, lo=0, hi=HALF):
            cols = slice(h * HALF + lo, h * HALF + hi)
            nc.scalar.activation(out=sgn[:, ot, cols], in_=ws[:, ot, cols], func=ACT.Sign)

        def scaled(gs, ot, h, lo, hi):
            nc.vector.scalar_tensor_tensor(
                out=gs[:, lo:hi],
                in0=acc[ot][h][:, lo:hi],
                scalar=1.0 / 255.0,
                in1=sgn[:, ot, h * HALF + lo : h * HALF + hi],
                op0=MULT,
                op1=MULT,
            )

        def expand(planes, gs, lo, hi, count):
            nc.vector.tensor_tensor(
                out=planes[:, :, 0:count],
                in0=gs[:, lo:hi].unsqueeze(2).to_broadcast([P, hi - lo, count]),
                in1=e8[:, 0:count].unsqueeze(1).to_broadcast([P, hi - lo, count]),
                op=MULT,
            )

        def low_planes(planes, on_gpsimd):
            if on_gpsimd:
                nc.gpsimd.tensor_scalar(
                    out=planes[:, :, 4:8],
                    in0=planes[:, :, 0:4],
                    scalar1=1.0 / 16.0,
                    scalar2=1.0,
                    op0=MULT,
                    op1=MULT,
                )
            else:
                nc.scalar.activation(
                    out=planes[:, :, 4:8], in_=planes[:, :, 0:4], func=ACT.Copy, scale=1.0 / 16.0
                )

        def store(planes, ot, h, lo, hi):
            nc.sync.dma_start(
                out=out[ot * P : (ot + 1) * P, h * HALF + lo : h * HALF + hi, :], in_=planes
            )

        def new_gs(ot, h, lo=0, hi=HALF):
            gs = gsp.tile([P, HALF], F32, name="gs")
            scaled(gs, ot, h, lo, hi)
            return gs

        S, G, SG = (False,), (True,), (False, True)

        def piece(gs, ot, h, lo, hi, lows):
            tile = smallp.tile([P, hi - lo, NBITS], F32, name="small")
            share = (hi - lo) // len(lows)
            for k, on_gpsimd in enumerate(lows):
                part = tile[:, k * share : (k + 1) * share, :]
                expand(part, gs, lo + k * share, lo + (k + 1) * share, 4)
                low_planes(part, on_gpsimd)
            store(tile[:], ot, h, lo, hi)

        def new_piece(width):
            return hp.tile([P, width, NBITS], F32, name="piece")

        def part(tile, gs, base, lo, hi, low):
            planes = tile[:, lo - base : hi - base, :]
            expand(planes, gs, lo, hi, 4)
            low_planes(planes, low[0])

        def on_gpsimd(planes, gs, lo, hi):
            nc.gpsimd.tensor_tensor(
                out=planes[:, :, 0:4],
                in0=gs[:, lo:hi].unsqueeze(2).to_broadcast([P, hi - lo, 4]),
                in1=e_sb[:].unsqueeze(1).to_broadcast([P, hi - lo, 4]),
                op=MULT,
            )
            low_planes(planes, True)

        def half_of(big, gs, lo, low):
            expand(big[:, lo : lo + 256, :], gs, lo, lo + 256, 4)
            low_planes(big[:, lo : lo + 256, :], low[0])

        def halves(big, gs, lows):
            half_of(big, gs, 0, lows[0])
            half_of(big, gs, 256, lows[1])

        vector_copy = nc.vector.tensor_copy
        scalar_copy = nc.scalar.copy
        e_sb = keep.tile([P, 4], F32, name="e_sb")
        nc.vector.tensor_copy(out=e_sb[:], in_=e8[:, 0:4])
        both = ((vector_copy, 0, 256), (scalar_copy, 256, HALF))

        pending = []

        def prepare(kind, c):
            raw = raw_g[c] if kind == "g" else raw_x[c][0]
            pending.append((kind, c, regroup(raw, both)))

        def finish():
            kind, c, grp = pending.pop(0)
            if kind == "g":
                quantise_g(grp, c, 0, OUT)
            else:
                quantise_x(grp, c, 0)
            if kind == "x" and c < 2:
                multiply(c, 0, range(O_TILES), 0, PASSES - 1)

        for i, (kind, c) in enumerate(HEAD):
            prepare(kind, c)
            if i > 0:
                finish()
        last = PASSES - 1
        every = range(O_TILES)
        grp_g = [None, None]
        grp_g[0] = regroup(raw_g[2], ((vector_copy, 0, 128), (scalar_copy, 128, HALF)))
        finish()
        quantise_g(grp_g[0], 2, 0, 128)
        multiply(2, 0, (0,), 0, last)
        sign(0, 0)
        grp_g[1] = regroup(raw_g[3], ((vector_copy, 0, 128), (scalar_copy, 256, HALF)))
        quantise_g(grp_g[1], 3, 0, 128)
        multiply(3, 0, (0,), 0, last)
        interleave(vector_copy, grp_g[1], raw_g[3], 128, 256)
        quantise_g(grp_g[0], 2, 128, 256)
        gs0 = new_gs(0, 0, 0, 64)
        quantise_g(grp_g[1], 3, 128, 256)
        for c in (2, 3):
            multiply(c, 0, (1,), 0, last)
        piece(gs0, 0, 0, 0, 64, S)
        sign(1, 0)
        scaled(gs0, 0, 0, 64, 256)
        scaled(gs0, 0, 0, 256, 512)
        piece(gs0, 0, 0, 64, 128, S)
        piece(gs0, 0, 0, 128, 256, S)
        grp_r = [new_grp() for c in range(PASSES)]
        turned = [turn(raw_x[3][1], 0, "bank7"), turn(raw_x[3][1], 1, "bank5")]
        tile = new_piece(256)
        part(tile, gs0, 256, 256, 384, S)
        part(tile, gs0, 256, 384, 512, S)
        store(tile[:], 0, 0, 256, 512)
        sign(2, 0)
        for c in (2, 3):
            quantise_g(grp_g[c - 2], c, 256, 512)
        for ot in (2, 3):
            for c in (2, 3):
                multiply(c, 0, (ot,), 0, last)
        gs1 = new_gs(1, 0)
        tile_a = new_piece(256)
        tile_b = new_piece(256)
        on_gpsimd(tile_b[:, 128:256, :], gs1, 384, 512)
        collect(turned[0], grp_r[3], 0)
        part(tile_a, gs1, 0, 0, 128, S)
        part(tile_a, gs1, 0, 128, 256, S)
        store(tile_a[:], 1, 0, 0, 256)
        sign(3, 0)
        gs2 = new_gs(2, 0)
        part(tile_b, gs1, 256, 256, 384, S)
        store(tile_b[:], 1, 0, 256, 512)
        collect(turned[1], grp_r[3], 1)
        turned = [turn(raw_x[0][1], 0, "bank6"), turn(raw_x[0][1], 1, "bank1")]
        whole2 = wholep.tile([P, HALF, NBITS], F32, name="whole")
        on_gpsimd(whole2[:, 384:512, :], gs2, 384, 512)
        part(whole2, gs2, 0, 0, 256, S)
        gs3 = new_gs(3, 0)
        part(whole2, gs2, 0, 256, 384, G)
        store(whole2[:], 2, 0, 0, HALF)
        collect(turned[0], grp_r[0], 0)
        collect(turned[1], grp_r[0], 1)
        turned = [turn(raw_x[2][1], 0, "bank7"), turn(raw_x[2][1], 1, "bank5")]
        interleave(scalar_copy, grp_r[1], raw_x[1][1], 256, 512)
        whole3 = wholep.tile([P, HALF, NBITS], F32, name="whole")
        half_of(whole3[:], gs3, 0, S)
        collect(turned[0], grp_r[2], 0)
        collect(turned[1], grp_r[2], 1)
        for ot in range(O_TILES):
            bank = psum.tile([P, HALF], F32, name="acc%d1" % ot, tag="bank%d" % RIGHT_BANKS[ot])
            acc[ot][1] = bank
        half_of(whole3[:], gs3, 256, S)
        store(whole3[:], 3, 0, 0, HALF)
        sign(0, 1)
        interleave(vector_copy, grp_r[1], raw_x[1][1], 0, 256)
        for c in (3, 0, 1, 2):
            quantise_x(grp_r[c], c, 1)
        for ot in every:
            for c in (3, 0, 1, 2):
                multiply(c, 1, (ot,), 3, 2)
        sign(1, 1)
        sign(2, 1)
        gs0 = new_gs(0, 1)
        whole0 = wholep.tile([P, HALF, NBITS], F32, name="whole")
        on_gpsimd(whole0[:, 384:512, :], gs0, 384, 512)
        part(whole0, gs0, 0, 0, 256, S)
        gs1 = new_gs(1, 1)
        part(whole0, gs0, 0, 256, 384, S)
        store(whole0[:], 0, 1, 0, HALF)
        sign(3, 1)
        whole1 = wholep.tile([P, HALF, NBITS], F32, name="whole")
        on_gpsimd(whole1[:, 384:512, :], gs1, 384, 512)
        part(whole1, gs1, 0, 0, 256, S)
        gs2 = new_gs(2, 1)
        part(whole1, gs1, 0, 256, 384, S)
        store(whole1[:], 1, 1, 0, HALF)
        pair = bigp.tile([P, 2, HALF, NBITS], F32, name="pair")
        on_gpsimd(pair[:, 0, 384:512, :], gs2, 384, 512)
        part(pair[:, 0, :, :], gs2, 0, 0, 256, S)
        gs3 = new_gs(3, 1)
        part(pair[:, 0, :, :], gs2, 0, 256, 384, S)
        on_gpsimd(pair[:, 1, 384:512, :], gs3, 384, 512)
        part(pair[:, 1, :, :], gs3, 0, 0, 256, S)
        part(pair[:, 1, :, :], gs3, 0, 256, 384, S)
        nc.sync.dma_start(out=out_view[:, 2:4, HALF:IN, :], in_=pair[:])
